import numpy as np
import ml_dtypes


def mxq(x, axis, fmt="e4m3"):
    dtype, down = {"e4m3": (ml_dtypes.float8_e4m3fn, 7), "e5m2": (ml_dtypes.float8_e5m2, 14)}[fmt]
    v = np.moveaxis(np.asarray(x, np.float32).astype(ml_dtypes.bfloat16).astype(np.float64), axis, -1)
    blocks = v.reshape(v.shape[:-1] + (-1, 32))
    amax = np.abs(blocks).max(-1, keepdims=True)
    byte = np.maximum(np.where(amax > 0, np.frexp(amax)[1] - 1 + 127, 0) - down, 1)
    scale = np.exp2(byte - 127.0)
    codes = (blocks / scale).astype(np.float32).astype(dtype).astype(np.float64)
    return np.moveaxis((codes * scale).reshape(v.shape), -1, axis)


WIDE = False


def mx_kscale(k):
    if not WIDE:
        return np.ones(k)
    levels = np.array([18, -18])
    if k % 512:
        return np.exp2(np.random.permutation(np.resize(levels, k // 32))).repeat(32)
    a = np.empty((k // 512, 16))
    for p in range(k // 512):
        a[p, :8] = np.random.permutation(np.resize(levels, 8))
        for g in range(8):
            far = levels[np.abs(levels - a[p, g]) >= 10]
            a[p, g + 8] = far[np.random.randint(len(far))]
    return np.exp2(a.ravel()).repeat(32)


BF16 = ml_dtypes.bfloat16


def bf(x):
    return np.asarray(x, np.float32).astype(BF16)


def f64(x):
    return np.asarray(x).astype(np.float64)


B, DI, DH = 1024, 384, 512


def sigmoid(v):
    return 1.0 / (1.0 + np.exp(-v))


def preacts(x, h_minors, s0, s1, s2, weight_ih, bias_ih, weight_hh, bias_hh,
            weight_sh0, bias_sh0, weight_sh1, bias_sh1, weight_sh2, bias_sh2):
    tmp = f64(x) @ f64(weight_ih).T + f64(bias_ih)
    tmp2 = f64(h_minors) @ f64(weight_hh).T + f64(bias_hh)
    tmp3 = np.concatenate([
        f64(s0) @ f64(weight_sh0).T + f64(bias_sh0),
        f64(s1) @ f64(weight_sh1).T + f64(bias_sh1),
        f64(s2) @ f64(weight_sh2).T + f64(bias_sh2),
    ], axis=1)
    return tmp[:, :4 * DH] + tmp2, tmp[:, 4 * DH:] + tmp3


def setup_inputs():
    s = mx_kscale(B)[:, None]
    u = mx_kscale(DH)
    n = np.random.standard_normal
    a, c = 0.7 / np.sqrt(DI), 0.7 / np.sqrt(DH)
    keep = np.random.uniform(size=B) < 0.9
    d = {
        "x": bf(n((B, DI))),
        "h_minors": bf(n((B, DH))),
        "c_minors": bf(n((B, DH))),
        "s0": bf(n((B, DH))),
        "s1": bf(n((B, DH))),
        "s2": bf(n((B, DH))),
        "mask": bf(keep * (0.5 + 0.5 * np.random.uniform(size=B))),
        "weight_ih": bf(n((7 * DH, DI)) * a),
        "bias_ih": bf(n(7 * DH) * 0.3),
        "weight_hh": bf(n((4 * DH, DH)) * c),
        "bias_hh": bf(n(4 * DH) * 0.3),
        "weight_sh0": bf(n((DH, DH)) * c),
        "bias_sh0": bf(n(DH) * 0.3),
        "weight_sh1": bf(n((DH, DH)) * c),
        "bias_sh1": bf(n(DH) * 0.3),
        "weight_sh2": bf(n((DH, DH)) * c),
        "bias_sh2": bf(n(DH) * 0.3),
    }
    pre, pre_s = preacts(d["x"], d["h_minors"], d["s0"], d["s1"], d["s2"], d["weight_ih"], d["bias_ih"],
                         d["weight_hh"], d["bias_hh"], d["weight_sh0"], d["bias_sh0"],
                         d["weight_sh1"], d["bias_sh1"], d["weight_sh2"], d["bias_sh2"])
    d["pre"] = np.asarray(pre, np.float32)
    d["pre_s"] = np.asarray(pre_s, np.float32)
    d["x"] = bf(f64(d["x"]) * s)
    d["weight_ih"] = bf(f64(d["weight_ih"]) / np.tile(u, 7)[:, None])
    for k in range(5):
        d["grad_%d" % k] = bf(n((B, DH)) * np.exp2(np.random.randint(-6, 1, (B, 1))) * 4.0 / s * u)
    return d


def reference(x, h_minors, c_minors, s0, s1, s2, mask, weight_ih, bias_ih, weight_hh, bias_hh,
              weight_sh0, bias_sh0, weight_sh1, bias_sh1, weight_sh2, bias_sh2,
              pre, pre_s, grad_0, grad_1, grad_2, grad_3, grad_4):
    d = DH
    m = f64(mask)[:, None]
    g_h, g_c, g_0, g_1, g_2 = f64(grad_0), f64(grad_1), f64(grad_2), f64(grad_3), f64(grad_4)

    p, ps = f64(pre), f64(pre_s)
    i_g, f_g, o_g = sigmoid(p[:, :d]), sigmoid(p[:, d:2 * d]), sigmoid(p[:, 2 * d:3 * d])
    ch = np.tanh(p[:, 3 * d:])
    b0, b1, b2 = sigmoid(ps[:, :d]), sigmoid(ps[:, d:2 * d]), sigmoid(ps[:, 2 * d:])
    t = np.tanh((f_g * f64(c_minors) + i_g * ch) * m)
    tc = t * m
    a0 = b0 + 1.0 - o_g
    s_0 = a0 * tc
    a1 = b1 + 2.0 - o_g - s_0
    s_1 = a1 * 0.5 * tc
    a2 = b2 + 3.0 - o_g - (2.0 * s_0 + s_1)

    da2 = g_2 * tc * (1.0 / 3.0)
    e1 = g_1 - da2
    da1 = e1 * 0.5 * tc
    e0 = g_0 - 2.0 * da2 - da1
    da0 = e0 * tc
    dtc = g_h * o_g + e0 * a0 + e1 * 0.5 * a1 + g_2 * a2 * (1.0 / 3.0)
    do = g_h * tc - da0 - da1 - da2
    q = (g_c + dtc * m * (1.0 - t * t)) * m
    dz = np.concatenate([
        q * ch * i_g * (1.0 - i_g),
        q * f64(c_minors) * f_g * (1.0 - f_g),
        do * o_g * (1.0 - o_g),
        q * i_g * (1.0 - ch * ch),
        da0 * b0 * (1.0 - b0),
        da1 * b1 * (1.0 - b1),
        da2 * b2 * (1.0 - b2),
    ], axis=1)

    dx = mxq(dz, 1, "e5m2") @ mxq(f64(weight_ih), 0, "e4m3")
    dw = mxq(dz, 0, "e5m2").T @ mxq(f64(x), 0, "e4m3")
    return dx, dw

@@ -1,0 +1,394 @@
+from contextlib import ExitStack
+
+import concourse.mybir as mybir
+from concourse.masks import make_identity
+
+F32 = mybir.dt.float32
+BF16 = mybir.dt.bfloat16
+U32 = mybir.dt.uint32
+U8 = mybir.dt.uint8
+E4M3 = mybir.dt.float8_e4m3fn_x4
+E5M2 = mybir.dt.float8_e5m2_x4
+ADD = mybir.AluOpType.add
+SUB = mybir.AluOpType.subtract
+MUL = mybir.AluOpType.mult
+SIGMOID = mybir.ActivationFunctionType.Sigmoid
+TANH = mybir.ActivationFunctionType.Tanh
+SQUARE = mybir.ActivationFunctionType.Square
+COPY = mybir.ActivationFunctionType.Copy
+
+B, DI, DH, GATES = 1024, 384, 512, 7
+P = 128
+J = 4
+W = 128
+GROUPS = B // 512
+CHUNKS = DH // W
+UNITS = GATES * CHUNKS
+QUADS = UNITS // 4
+PAD = 128
+
+FLOPS = 2 * 2 * B * GATES * DH * DI
+BYTES = (
+    B * 4 * DH * 4 + B * 3 * DH * 4 + 6 * B * DH * 2 + B * 2 + B * DI * 2 + GATES * DH * DI * 2
+    + B * DI * 4 + GATES * DH * DI * 4
+)
+
+ORDER = [6, 5, 4, 2, 0, 1, 3]
+KSQ = (1.0 / 12.0) ** 0.5
+
+
+def tile_share_lstm_cell_pa_v_kernel(
+    tc, x, h_minors, c_minors, s0, s1, s2, mask, weight_ih, bias_ih, weight_hh, bias_hh,
+    weight_sh0, bias_sh0, weight_sh1, bias_sh1, weight_sh2, bias_sh2,
+    pre, pre_s, grad_0, grad_1, grad_2, grad_3, grad_4, out_0, out_1,
+):
+    nc = tc.nc
+    with ExitStack() as ctx:
+        keep = ctx.enter_context(tc.tile_pool(name="keep", bufs=1))
+        raw = ctx.enter_context(tc.tile_pool(name="raw", bufs=3))
+        act = ctx.enter_context(tc.tile_pool(name="act", bufs=2))
+        vec = ctx.enter_context(tc.tile_pool(name="vec", bufs=1))
+        dzp = ctx.enter_context(tc.tile_pool(name="dzp", bufs=2))
+        stage = ctx.enter_context(tc.tile_pool(name="stage", bufs=2))
+        tps = ctx.enter_context(tc.psum_pool(name="tps", bufs=4))
+        mps = ctx.enter_context(tc.psum_pool(name="mps", bufs=4))
+
+        ident = keep.tile([P, P], F32, name="ident")
+        make_identity(nc, ident[:])
+        warm = keep.tile([P, 1], F32, name="warm")
+        nc.vector.memset(warm[:], 0.0)
+        nc.scalar.activation(warm[:], warm[:], SIGMOID)
+
+        w_codes = keep.tile([P, QUADS * DI + PAD], U32, name="w_codes", align_bytes=64)
+        w_scales = keep.tile([P, QUADS * DI + PAD], U8, name="w_scales", align_bytes=64)
+        x_codes = keep.tile([P, GROUPS * DI + PAD], U32, name="x_codes", align_bytes=64)
+        x_scales = keep.tile([P, GROUPS * DI + PAD], U8, name="x_scales", align_bytes=64)
+        for codes, scales, used in ((w_codes, w_scales, QUADS * DI), (x_codes, x_scales, GROUPS * DI)):
+            nc.gpsimd.memset(codes[:, used : used + PAD], 0)
+            nc.gpsimd.memset(scales[:, used : used + PAD], 0)
+
+        m_raw = keep.tile([P, GROUPS, J], BF16, name="m_raw")
+        m32 = keep.tile([P, GROUPS * J], F32, name="m32")
+        msq6 = keep.tile([P, GROUPS * J], F32, name="msq6")
+
+        def mcol(tile, g, j):
+            return tile[:, g * J + j : g * J + j + 1]
+
+        st = {}
+
+        def tokens(src, g, col0, width):
+            return src[512 * g : 512 * (g + 1), col0 : col0 + width].rearrange("(p j) w -> p j w", j=J)
+
+        def load(n):
+            g, c = divmod(n, CHUNKS)
+            t = {}
+            for nm, src, col, dt in (
+                ("ig", pre, 0, F32), ("ch", pre, 3 * DH, F32), ("fg", pre, DH, F32), ("cm", c_minors, 0, BF16),
+                ("g4", grad_4, 0, BF16), ("g3", grad_3, 0, BF16), ("tb2", pre_s, 2 * DH, F32),
+                ("g0", grad_0, 0, BF16), ("g2", grad_2, 0, BF16), ("tb1", pre_s, DH, F32), ("tb0", pre_s, 0, F32),
+                ("to", pre, 2 * DH, F32), ("g1", grad_1, 0, BF16),
+            ):
+                tl = raw.tile([P, J, W], dt, name=nm, tag=nm)
+                nc.sync.dma_start(out=tl[:], in_=tokens(src, g, col + c * W, W))
+                t[nm] = tl
+            st[n] = t
+
+        def s_forward(n):
+            t = st[n]
+            for nm, fn in (("ig", SIGMOID), ("ch", TANH), ("fg", SIGMOID)):
+                nc.scalar.activation(t[nm][:], t[nm][:], fn)
+
+        def s_gates(n):
+            t = st[n]
+            g = n // CHUNKS
+            for nm, sc in (("tb2", 0.5), ("tb1", 0.5), ("tb0", 0.5), ("to", -0.5)):
+                nc.scalar.activation(t[nm][:], t[nm][:], TANH, scale=sc)
+                sq = act.tile([P, J, W], F32, name="q" + nm, tag="q" + nm)
+                nc.scalar.activation(sq[:], t[nm][:], SQUARE, scale=KSQ)
+                t["q" + nm] = sq
+            mg1 = act.tile([P, J, W], F32, name="mg1", tag="mg1")
+            for j in range(J):
+                nc.scalar.activation(mg1[:, j, :], t["g1"][:, j, :], COPY, scale=mcol(m32, g, j))
+            t["mg1"] = mg1
+            chq = act.tile([P, J, W], F32, name="chq", tag="chq")
+            nc.scalar.activation(chq[:], t["ch"][:], SQUARE)
+            t["chq"] = chq
+
+        def s_tanh(n):
+            t = st[n]
+            g = n // CHUNKS
+            tt = act.tile([P, J, W], F32, name="tt", tag="tt")
+            tau = act.tile([P, J, W], F32, name="tau", tag="tau")
+            for j in range(J):
+                nc.scalar.activation(tt[:, j, :], t["z"][:, j, :], TANH, scale=mcol(m32, g, j))
+            for j in range(J):
+                nc.scalar.activation(tau[:, j, :], tt[:, j, :], COPY, scale=mcol(m32, g, j))
+            pt = tps.tile([P, J, P], F32, name="ps", tag="ps")
+            flip(pt, [tt])
+            t2 = act.tile([P, J, P], F32, name="t2", tag="t2")
+            nc.scalar.activation(t2[:], pt[:], SQUARE)
+            t["tau"], t["t2"] = tau, t2
+
+        def flip(bank, terms):
+            for j in range(J):
+                for i, term in enumerate(terms):
+                    nc.tensor.matmul(
+                        bank[:, j, :], lhsT=term[:, j, :], rhs=ident[:], is_transpose=True,
+                        start=(i == 0), stop=(i == len(terms) - 1))
+
+        def vtile(n, nm, pool=None):
+            tl = (pool or vec).tile([P, J, W], F32, name=nm, tag=nm)
+            st[n][nm] = tl
+            return tl
+
+        def stt(out, a, s, b, op0, op1):
+            nc.vector.scalar_tensor_tensor(out=out[:], in0=a[:], scalar=s, in1=b[:], op0=op0, op1=op1)
+
+        def tt2(out, a, b, op):
+            nc.vector.tensor_tensor(out=out[:], in0=a[:], in1=b[:], op=op)
+
+        quad_tiles = {}
+
+        def unit_out(n, u):
+            g, c = divmod(n, CHUNKS)
+            q, kk = divmod(GATES * c + u, 4)
+            if kk == 0:
+                quad_tiles[g, q] = dzp.tile([P, J, 4, W], BF16, name="dz", tag="dz", bufs=3, align_bytes=64)
+            return quad_tiles[g, q][:, :, kk, :]
+
+        def final(n, u, sq, cst, val):
+            nc.vector.scalar_tensor_tensor(
+                out=unit_out(n, u), in0=sq[:], scalar=cst, in1=val[:], op0=ADD, op1=MUL)
+
+        def v_forward(n):
+            t = st[n]
+            a = vtile(n, "fc", act)
+            b = vtile(n, "ich", act)
+            z = vtile(n, "z", act)
+            return [
+                lambda: tt2(b, t["ig"], t["ch"], MUL),
+                lambda: tt2(a, t["fg"], t["cm"], MUL),
+                lambda: tt2(z, a, b, ADD),
+            ]
+
+        def v_main(n):
+            t = st[n]
+            g = n // CHUNKS
+            tau = t["tau"]
+            D2, E1, D1, E0, D0, H1, NT, G3, X, P1, P2 = (
+                vtile(n, nm) for nm in ("D2", "E1", "D1", "E0", "D0", "H1", "NT", "G3", "X", "P1", "P2"))
+            ops = []
+
+            def o(f, *args):
+                ops.append(lambda: f(*args))
+
+            o(stt, D2, t["g4"], -1.0, tau, MUL, MUL)
+            o(stt, G3, t["g0"], -3.0, t["g4"], MUL, ADD)
+            o(stt, E1, t["g3"], 3.0, D2, MUL, ADD)
+            o(stt, P2, t["tb2"], 7.0, t["g4"], ADD, MUL)
+            o(stt, D1, E1, -0.5, tau, MUL, MUL)
+            o(stt, H1, t["g3"], 1.5, D2, MUL, ADD)
+            o(stt, E0, D2, 2.0 / 3.0, t["g2"], MUL, ADD)
+            o(stt, NT, H1, -1.0, tau, MUL, MUL)
+            o(stt, E0, E0, 3.0, D1, MUL, ADD)
+            o(final, n, 0, t["qtb2"], -1.0 / 12.0, D2)
+            o(stt, NT, D2, 2.0, NT, MUL, ADD)
+            o(final, n, 1, t["qtb1"], -1.0 / 12.0, D1)
+            o(stt, D0, E0, -1.0, tau, MUL, MUL)
+            o(tt2, NT, NT, E0, ADD)
+            o(stt, X, E1, 0.5, G3, MUL, ADD)
+            o(tt2, G3, G3, H1, ADD)
+            o(tt2, X, X, E0, ADD)
+            o(final, n, 2, t["qtb0"], -1.0 / 12.0, D0)
+            o(tt2, G3, G3, NT, ADD)
+            o(tt2, X, X, tau, MUL)
+            o(stt, NT, t["tb0"], 3.0, NT, ADD, MUL)
+            o(stt, P1, t["tb1"], 5.0, H1, ADD, MUL)
+            o(stt, G3, t["to"], -1.0, G3, ADD, MUL)
+            dtc = tps.tile([P, J, P], F32, name="ps", tag="ps")
+            back = tps.tile([P, J, P], F32, name="ps", tag="ps")
+            o(flip, dtc, [P1, NT, P2, G3])
+            o(final, n, 3, t["qto"], -1.0 / 12.0, X)
+            o(stt, t["ich"], t["ig"], -1.0, t["ich"], ADD, MUL)
+            o(stt, D1, t["t2"], -1.0, dtc, ADD, MUL)
+            o(flip, back, [D1])
+            o(stt, t["fc"], t["fg"], -1.0, t["fc"], ADD, MUL)
+
+            def qn(j):
+                nc.vector.scalar_tensor_tensor(
+                    out=P1[:, j, :], in0=back[:, j, :], scalar=mcol(msq6, g, j), in1=t["mg1"][:, j, :],
+                    op0=MUL, op1=SUB)
+
+            o(stt, t["chq"], t["chq"], -1.0, t["ig"], ADD, MUL)
+            for j in range(J):
+                o(qn, j)
+            o(lambda: nc.vector.tensor_tensor(out=unit_out(n, 4), in0=P1[:], in1=t["ich"][:], op=MUL))
+            o(lambda: nc.vector.tensor_tensor(out=unit_out(n, 5), in0=P1[:], in1=t["fc"][:], op=MUL))
+            o(lambda: nc.vector.tensor_tensor(out=unit_out(n, 6), in0=P1[:], in1=t["chq"][:], op=MUL))
+            return ops
+
+        tok = {}
+        feat = {}
+
+        def quad_spread(g, q):
+            dz = quad_tiles[g, q]
+            inter = dzp.tile([P, 4 * W, J], BF16, name="inter", tag="inter", align_bytes=64)
+            nc.scalar.copy(inter[:], dz[:].rearrange("p j k w -> p (k w) j"))
+            words = dz[:].rearrange("p j k w -> p (j k w)").bitcast(F32)
+            fz = dzp.tile([P, 4 * P, J], BF16, name="fz", tag="fz", align_bytes=64)
+            fw = fz[:].rearrange("p n t -> p (n t)").bitcast(F32).rearrange("p (h a n u) -> p h a n u", h=2, a=2, u=2)
+            for h in range(2):
+                ps = tps.tile([P, 2, 2, P], F32, name="ps", tag="ps")
+                for a in range(2):
+                    for u in range(2):
+                        lo = 256 * (2 * h + a)
+                        nc.tensor.transpose(ps[:, a, u, :], words[:, lo + u : lo + 256 : 2], ident[:])
+                nc.scalar.copy(fw[:, h], ps[:].rearrange("p a u n -> p a n u"))
+            return inter, fz
+
+        def quad_quantize(g, q, inter, fz):
+            tc_ = keep.tile([P, 4 * W], U32, name="tokc%d" % q, tag="tokc%d_%d" % (g, q) if g == 0 else "tokc1_%d" % (q % 2), align_bytes=64)
+            ts_ = keep.tile([P, 4 * W], U8, name="toks%d" % q, tag="toks%d_%d" % (g, q) if g == 0 else "toks1_%d" % (q % 2), align_bytes=64)
+            fc_ = keep.tile([P, 4 * P], U32, name="featc%d" % q, tag="featc%d" % q, align_bytes=64)
+            fs_ = keep.tile([P, 4 * P], U8, name="feats%d" % q, tag="feats%d" % q, align_bytes=64)
+            tok[g, q] = (tc_, ts_)
+            feat[g, q] = (fc_, fs_)
+            return [
+                lambda: nc.vector.quantize_mx(
+                    out=tc_[:].bitcast(E5M2), scales=ts_[:], in_=inter[:].rearrange("p w j -> p (w j)")),
+                lambda: nc.vector.quantize_mx(
+                    out=fc_[:].bitcast(E5M2), scales=fs_[:], in_=fz[:].rearrange("p n t -> p (n t)")),
+            ]
+
+        def quad_weight_grad(q):
+            for kk in range(4):
+                unit = 4 * q + kk
+                c, u = divmod(unit, GATES)
+                row = DH * ORDER[u] + W * c
+                acc = mps.tile([P, 512], F32, name="acc", tag="acc")
+                for g in range(GROUPS):
+                    codes, scales = tok[g, q]
+                    nc.tensor.matmul_mx(
+                        out=acc[:],
+                        lhsT=codes[:, W * kk : W * (kk + 1)].bitcast(E5M2),
+                        lhsT_scale=scales[:, W * kk : W * (kk + 1)],
+                        rhs=x_codes[:, DI * g : DI * g + 512].bitcast(E4M3),
+                        rhs_scale=x_scales[:, DI * g : DI * g + 512],
+                        start=(g == 0), stop=(g == GROUPS - 1),
+                    )
+                res = stage.tile([P, DI], F32, name="res", tag="res", bufs=4)
+                nc.scalar.copy(res[:], acc[:, :DI])
+                nc.sync.dma_start(out=out_1[row : row + W, :], in_=res[:])
+
+        def data_grad(g):
+            rows = out_0[512 * g : 512 * (g + 1), :].rearrange("(p j) d -> p j d", j=J)
+            for j in range(J):
+                acc = mps.tile([P, 512], F32, name="acc", tag="acc")
+                for q in range(QUADS):
+                    codes, scales = feat[g, q]
+                    nc.tensor.matmul_mx(
+                        out=acc[:],
+                        lhsT=codes[:, P * j : P * (j + 1)].bitcast(E5M2),
+                        lhsT_scale=scales[:, P * j : P * (j + 1)],
+                        rhs=w_codes[:, DI * q : DI * q + 512].bitcast(E4M3),
+                        rhs_scale=w_scales[:, DI * q : DI * q + 512],
+                        start=(q == 0), stop=(q == QUADS - 1),
+                    )
+                res = stage.tile([P, DI], F32, name="res", tag="res", bufs=4)
+                nc.scalar.copy(res[:], acc[:, :DI])
+                nc.sync.dma_start(out=rows[:, j, :], in_=res[:])
+
+        def load_w(q):
+            wr = stage.tile([P, J, DI], BF16, name="wr", tag="wr")
+            for kk in range(4):
+                c, u = divmod(4 * q + kk, GATES)
+                row = DH * ORDER[u] + W * c
+                nc.sync.dma_start(
+                    out=wr[32 * kk : 32 * (kk + 1), :, :],
+                    in_=weight_ih[row : row + W, :].rearrange("(r j) d -> r j d", j=J))
+            return wr
+
+        def load_x(g):
+            xr = stage.tile([P, J, DI], BF16, name="wr", tag="wr")
+            nc.sync.dma_start(out=xr[:], in_=tokens(x, g, 0, DI))
+            return xr
+
+        def group4(src):
+            grp = stage.tile([P, DI, J], BF16, name="grp", tag="grp", align_bytes=64)
+            nc.scalar.copy(grp[:], src[:].rearrange("p j d -> p d j"))
+            return grp
+
+        def quant4(grp, codes, scales, col):
+            flat = grp[:].rearrange("p d j -> p (d j)")
+            return [
+                lambda: nc.vector.quantize_mx(
+                    out=codes[:, col : col + 256].bitcast(E4M3), scales=scales[:, col : col + 256], in_=flat[:, :1024]),
+                lambda: nc.vector.quantize_mx(
+                    out=codes[:, col + 256 : col + DI].bitcast(E4M3), scales=scales[:, col + 256 : col + DI],
+                    in_=flat[:, 1024:]),
+            ]
+
+        def quads_done(c):
+            return [q for q in range(QUADS) if GATES * c <= 4 * q + 3 < GATES * (c + 1)]
+
+        with tc.manual_schedule():
+            nc.sync.dma_start(out=m_raw[:], in_=mask.rearrange("(g p j) -> p g j", g=GROUPS, j=J))
+            load(0)
+            nc.vector.tensor_copy(out=m32[:], in_=m_raw[:].rearrange("p g j -> p (g j)"))
+            nc.vector.scalar_tensor_tensor(out=msq6[:], in0=m32[:], scalar=1.0 / 6.0, in1=m32[:], op0=MUL, op1=MUL)
+            load(1)
+            s_forward(0)
+            for f in v_forward(0):
+                f()
+            s_gates(0)
+            s_tanh(0)
+
+            operands = [("x", 0), ("x", 1)] + [("w", q) for q in range(QUADS)]
+            pending = []
+            for n in range(GROUPS * CHUNKS):
+                g, c = divmod(n, CHUNKS)
+                last = n == GROUPS * CHUNKS - 1
+                if n + 2 < GROUPS * CHUNKS:
+                    load(n + 2)
+                if not last:
+                    s_forward(n + 1)
+                ops = v_main(n)
+                fwd = [] if last else v_forward(n + 1)
+                small = []
+                if g == 0:
+                    take = 3 if c < 3 else 0
+                    for _ in range(take):
+                        kind, i = operands.pop(0)
+                        if kind == "x":
+                            small += quant4(group4(load_x(i)), x_codes, x_scales, DI * i)
+                        else:
+                            small += quant4(group4(load_w(i)), w_codes, w_scales, DI * i)
+                extra = {}
+                for i, f in enumerate(pending):
+                    extra.setdefault(4 + 3 * i, []).append(f)
+                for i, f in enumerate(fwd):
+                    extra.setdefault(12 + 2 * i, []).append(f)
+                for i, f in enumerate(small):
+                    extra.setdefault(19 + 2 * i, []).append(f)
+                for i, f in enumerate(ops):
+                    f()
+                    for e in extra.get(i, []):
+                        e()
+                    if i == 16 and not last:
+                        s_gates(n + 1)
+                        s_tanh(n + 1)
+                if g == 1 and c == 0:
+                    data_grad(0)
+                if g == 1 and c >= 1:
+                    for q in quads_done(c - 1):
+                        quad_weight_grad(q)
+                pending = []
+                for q in quads_done(c):
+                    inter, fz = quad_spread(g, q)
+                    pending += quad_quantize(g, q, inter, fz)
+                if last:
+                    for f in pending:
+                        f()
+                    for q in quads_done(c):
+                        quad_weight_grad(q)
+                    data_grad(1)

@@ -34,7 +34,19 @@ BYTES = (
 )
 
 ORDER = [6, 5, 4, 2, 0, 1, 3]
-KSQ = (1.0 / 12.0) ** 0.5
+K6 = (1.0 / 6.0) ** 0.5
+K12 = (1.0 / 12.0) ** 0.5
+N = GROUPS * CHUNKS
+PERIOD = [
+    ("Fdtc", -1), ("fq", 0), ("fcg", 0), ("gb2", 0), ("fgB", 0), ("D2", 0), ("bk", -1), ("x", 0), ("E1", 0), ("x", 0),
+    ("gto", 0), ("U", 0), ("D1", 0), ("Fb2", 0), ("b2", 0), ("sfwd", 1), ("x", 0), ("M", 0), ("Fback", -1), ("Fb1", 0),
+    ("H1", 0), ("E0", 0), ("x", 0), ("x", 0), ("G", 0), ("grp", 0), ("Fh1", 0), ("q", -1), ("b1", 0), ("df", -1),
+    ("P1", 0), ("di", -1), ("x", 0), ("tq", 0), ("dc", -1), ("gb1", 1), ("NG", 0), ("half", 0), ("gb0", 1), ("Fh0", 0),
+    ("fgA", 1), ("load", 2), ("Fy", 0), ("half", 0), ("wq", 0), ("t2", 0), ("D0", 0), ("fc", 1), ("ich", 1), ("half", 0),
+    ("Fb0", 0), ("P0", 0), ("Fdo", 0), ("Fz", 1), ("PO", 0), ("tanh", 1), ("x", 0), ("P2", 0), ("tq", 0), ("b0", 0),
+    ("fq", 0), ("tq", 0), ("wq", 0), ("fo", 0), ("x", 0), ("chq", 1), ("fi", 1), ("ff", 1), ("x", 0), ("tau", 1),
+    ("half", 0), ("grp", 0),
+]
 
 
 def tile_share_lstm_cell_pa_v_kernel(
@@ -50,11 +62,14 @@ def tile_share_lstm_cell_pa_v_kernel(
         vec = ctx.enter_context(tc.tile_pool(name="vec", bufs=1))
         dzp = ctx.enter_context(tc.tile_pool(name="dzp", bufs=2))
         stage = ctx.enter_context(tc.tile_pool(name="stage", bufs=2))
-        tps = ctx.enter_context(tc.psum_pool(name="tps", bufs=4))
-        mps = ctx.enter_context(tc.psum_pool(name="mps", bufs=4))
+        gps = ctx.enter_context(tc.psum_pool(name="gps", bufs=2))
+        fps = ctx.enter_context(tc.psum_pool(name="fps", bufs=4))
+        mps = ctx.enter_context(tc.psum_pool(name="mps", bufs=2))
 
         ident = keep.tile([P, P], F32, name="ident")
         make_identity(nc, ident[:])
+        ident_bf = keep.tile([P, P], BF16, name="ident_bf")
+        make_identity(nc, ident_bf[:])
         warm = keep.tile([P, 1], F32, name="warm")
         nc.vector.memset(warm[:], 0.0)
         nc.scalar.activation(warm[:], warm[:], SIGMOID)
@@ -69,7 +84,8 @@ def tile_share_lstm_cell_pa_v_kernel(
 
         m_raw = keep.tile([P, GROUPS, J], BF16, name="m_raw")
         m32 = keep.tile([P, GROUPS * J], F32, name="m32")
-        msq6 = keep.tile([P, GROUPS * J], F32, name="msq6")
+        m6 = keep.tile([P, GROUPS * J], F32, name="m6")
+        m_bc = keep.tile([P, GROUPS, J, P], BF16, name="m_bc")
 
         def mcol(tile, g, j):
             return tile[:, g * J + j : g * J + j + 1]
@@ -79,316 +95,313 @@ def tile_share_lstm_cell_pa_v_kernel(
         def tokens(src, g, col0, width):
             return src[512 * g : 512 * (g + 1), col0 : col0 + width].rearrange("(p j) w -> p j w", j=J)
 
+        LOADS = (
+            ("ig", pre, 0, F32), ("ch", pre, 3 * DH, F32), ("fg", pre, DH, F32), ("cm", c_minors, 0, BF16),
+            ("g4", grad_4, 0, BF16), ("g0", grad_0, 0, BF16), ("g3", grad_3, 0, BF16), ("g2", grad_2, 0, BF16),
+            ("tb2", pre_s, 2 * DH, F32), ("tb1", pre_s, DH, F32), ("tb0", pre_s, 0, F32),
+            ("to", pre, 2 * DH, F32), ("g1", grad_1, 0, BF16),
+        )
+
         def load(n):
             g, c = divmod(n, CHUNKS)
             t = {}
-            for nm, src, col, dt in (
-                ("ig", pre, 0, F32), ("ch", pre, 3 * DH, F32), ("fg", pre, DH, F32), ("cm", c_minors, 0, BF16),
-                ("g4", grad_4, 0, BF16), ("g3", grad_3, 0, BF16), ("tb2", pre_s, 2 * DH, F32),
-                ("g0", grad_0, 0, BF16), ("g2", grad_2, 0, BF16), ("tb1", pre_s, DH, F32), ("tb0", pre_s, 0, F32),
-                ("to", pre, 2 * DH, F32), ("g1", grad_1, 0, BF16),
-            ):
-                tl = raw.tile([P, J, W], dt, name=nm, tag=nm)
+            for nm, src, col, dt in LOADS:
+                tl = raw.tile([P, J, W], dt, name=nm, tag=nm, bufs=2 if nm in ("cm", "g0", "g3", "g2") else 3)
                 nc.sync.dma_start(out=tl[:], in_=tokens(src, g, col + c * W, W))
                 t[nm] = tl
             st[n] = t
 
-        def s_forward(n):
-            t = st[n]
-            for nm, fn in (("ig", SIGMOID), ("ch", TANH), ("fg", SIGMOID)):
-                nc.scalar.activation(t[nm][:], t[nm][:], fn)
-
-        def s_gates(n):
-            t = st[n]
-            g = n // CHUNKS
-            for nm, sc in (("tb2", 0.5), ("tb1", 0.5), ("tb0", 0.5), ("to", -0.5)):
-                nc.scalar.activation(t[nm][:], t[nm][:], TANH, scale=sc)
-                sq = act.tile([P, J, W], F32, name="q" + nm, tag="q" + nm)
-                nc.scalar.activation(sq[:], t[nm][:], SQUARE, scale=KSQ)
-                t["q" + nm] = sq
-            mg1 = act.tile([P, J, W], F32, name="mg1", tag="mg1")
-            for j in range(J):
-                nc.scalar.activation(mg1[:, j, :], t["g1"][:, j, :], COPY, scale=mcol(m32, g, j))
-            t["mg1"] = mg1
-            chq = act.tile([P, J, W], F32, name="chq", tag="chq")
-            nc.scalar.activation(chq[:], t["ch"][:], SQUARE)
-            t["chq"] = chq
-
-        def s_tanh(n):
-            t = st[n]
-            g = n // CHUNKS
-            tt = act.tile([P, J, W], F32, name="tt", tag="tt")
-            tau = act.tile([P, J, W], F32, name="tau", tag="tau")
-            for j in range(J):
-                nc.scalar.activation(tt[:, j, :], t["z"][:, j, :], TANH, scale=mcol(m32, g, j))
-            for j in range(J):
-                nc.scalar.activation(tau[:, j, :], tt[:, j, :], COPY, scale=mcol(m32, g, j))
-            pt = tps.tile([P, J, P], F32, name="ps", tag="ps")
-            flip(pt, [tt])
-            t2 = act.tile([P, J, P], F32, name="t2", tag="t2")
-            nc.scalar.activation(t2[:], pt[:], SQUARE)
-            t["tau"], t["t2"] = tau, t2
-
-        def flip(bank, terms):
-            for j in range(J):
-                for i, term in enumerate(terms):
-                    nc.tensor.matmul(
-                        bank[:, j, :], lhsT=term[:, j, :], rhs=ident[:], is_transpose=True,
-                        start=(i == 0), stop=(i == len(terms) - 1))
-
-        def vtile(n, nm, pool=None):
-            tl = (pool or vec).tile([P, J, W], F32, name=nm, tag=nm)
+        def new(n, nm, pool, dt=F32):
+            tl = pool.tile([P, J, W], dt, name=nm, tag=nm)
             st[n][nm] = tl
             return tl
 
         def stt(out, a, s, b, op0, op1):
             nc.vector.scalar_tensor_tensor(out=out[:], in0=a[:], scalar=s, in1=b[:], op0=op0, op1=op1)
 
-        def tt2(out, a, b, op):
+        def mul(out, a, b, op=MUL):
             nc.vector.tensor_tensor(out=out[:], in0=a[:], in1=b[:], op=op)
 
+        def flip(n, nm, *terms):
+            bank = fps.tile([P, J, P], F32, name="flipped", tag="flipped")
+            for j in range(J):
+                for i, term in enumerate(terms):
+                    nc.tensor.matmul(
+                        bank[:, j, :], lhsT=st[n][term][:, j, :], rhs=ident[:], is_transpose=True,
+                        start=(i == 0), stop=(i == len(terms) - 1))
+            st[n][nm] = bank
+
+        def per_j(fn):
+            for j in range(J):
+                fn(j)
+
+        def s_forward(n):
+            t = st[n]
+            g = n // CHUNKS
+            im = new(n, "im", act)
+            nc.scalar.activation(t["ig"][:], t["ig"][:], SIGMOID)
+            for j in range(J):
+                nc.scalar.activation(im[:, j, :], t["ig"][:, j, :], COPY, scale=mcol(m32, g, j))
+            nc.scalar.activation(t["ch"][:], t["ch"][:], TANH)
+            nc.scalar.activation(t["fg"][:], t["fg"][:], SIGMOID)
+
+        def s_chq(n):
+            nc.scalar.activation(new(n, "chq", act)[:], st[n]["ch"][:], SQUARE)
+
+        def s_gate(n, nm):
+            t = st[n]
+            nc.scalar.activation(t[nm][:], t[nm][:], TANH, scale=-0.5 if nm == "to" else 0.5)
+            sq = new(n, "q" + nm, act)
+            nc.scalar.activation(sq[:], t[nm][:], SQUARE, scale=K6 if nm == "tb2" else K12)
+            if nm == "to":
+                nc.scalar.activation(sq[:], sq[:], COPY, scale=-1.0, bias=1.0 / 12.0)
+
+        def flip_pair(n, a, b):
+            t = st[n]
+            bank = gps.tile([P, 2, J, P], BF16, name="gb", tag="gb")
+            for i, nm in enumerate((a, b)):
+                for j in range(J):
+                    nc.tensor.transpose(bank[:, i, j, :], t[nm][:, j, :], ident_bf[:])
+                t[nm + "f"] = bank[:, i]
+            if b == "g0":
+                nc.scalar.copy(new(n, "g0s", act, BF16)[:], t["g0f"])
+
         quad_tiles = {}
+        tok = {}
+        feat = {}
 
         def unit_out(n, u):
             g, c = divmod(n, CHUNKS)
             q, kk = divmod(GATES * c + u, 4)
-            if kk == 0:
-                quad_tiles[g, q] = dzp.tile([P, J, 4, W], BF16, name="dz", tag="dz", bufs=3, align_bytes=64)
-            return quad_tiles[g, q][:, :, kk, :]
+            if (g, q) not in quad_tiles:
+                quad_tiles[g, q] = dzp.tile([P, 4, W, J], BF16, name="dz", tag="dz", bufs=4, align_bytes=64)
+            return quad_tiles[g, q][:, kk, :, :]
+
+        def inter(tile):
+            return tile[:].rearrange("p j w -> p w j")
 
         def final(n, u, sq, cst, val):
             nc.vector.scalar_tensor_tensor(
-                out=unit_out(n, u), in0=sq[:], scalar=cst, in1=val[:], op0=ADD, op1=MUL)
+                out=unit_out(n, u), in0=inter(sq), scalar=cst, in1=inter(val), op0=ADD, op1=MUL)
 
-        def v_forward(n):
-            t = st[n]
-            a = vtile(n, "fc", act)
-            b = vtile(n, "ich", act)
-            z = vtile(n, "z", act)
-            return [
-                lambda: tt2(b, t["ig"], t["ch"], MUL),
-                lambda: tt2(a, t["fg"], t["cm"], MUL),
-                lambda: tt2(z, a, b, ADD),
-            ]
+        def final2(n, u, a, b):
+            nc.vector.tensor_tensor(out=unit_out(n, u), in0=inter(a), in1=inter(b), op=MUL)
 
-        def v_main(n):
-            t = st[n]
-            g = n // CHUNKS
-            tau = t["tau"]
-            D2, E1, D1, E0, D0, H1, NT, G3, X, P1, P2 = (
-                vtile(n, nm) for nm in ("D2", "E1", "D1", "E0", "D0", "H1", "NT", "G3", "X", "P1", "P2"))
-            ops = []
+        def quad_half(g, q, h, fz):
+            words = quad_tiles[g, q][:].rearrange("p k w j -> p (k w j)").bitcast(F32)
+            ps = mps.tile([P, 4, P], F32, name="mb", tag="mb")
+            for t in range(4):
+                nc.tensor.transpose(ps[:, t, :], words[:, 2 * t + h :: 8], ident[:])
+            src = ps[:].rearrange("p t n -> p (t n)").bitcast(BF16).rearrange("p (t n e) -> p e n t", t=4, e=2)
+            nc.scalar.copy(fz[:, 2 * h : 2 * h + 2, :, :], src)
 
-            def o(f, *args):
-                ops.append(lambda: f(*args))
-
-            o(stt, D2, t["g4"], -1.0, tau, MUL, MUL)
-            o(stt, G3, t["g0"], -3.0, t["g4"], MUL, ADD)
-            o(stt, E1, t["g3"], 3.0, D2, MUL, ADD)
-            o(stt, P2, t["tb2"], 7.0, t["g4"], ADD, MUL)
-            o(stt, D1, E1, -0.5, tau, MUL, MUL)
-            o(stt, H1, t["g3"], 1.5, D2, MUL, ADD)
-            o(stt, E0, D2, 2.0 / 3.0, t["g2"], MUL, ADD)
-            o(stt, NT, H1, -1.0, tau, MUL, MUL)
-            o(stt, E0, E0, 3.0, D1, MUL, ADD)
-            o(final, n, 0, t["qtb2"], -1.0 / 12.0, D2)
-            o(stt, NT, D2, 2.0, NT, MUL, ADD)
-            o(final, n, 1, t["qtb1"], -1.0 / 12.0, D1)
-            o(stt, D0, E0, -1.0, tau, MUL, MUL)
-            o(tt2, NT, NT, E0, ADD)
-            o(stt, X, E1, 0.5, G3, MUL, ADD)
-            o(tt2, G3, G3, H1, ADD)
-            o(tt2, X, X, E0, ADD)
-            o(final, n, 2, t["qtb0"], -1.0 / 12.0, D0)
-            o(tt2, G3, G3, NT, ADD)
-            o(tt2, X, X, tau, MUL)
-            o(stt, NT, t["tb0"], 3.0, NT, ADD, MUL)
-            o(stt, P1, t["tb1"], 5.0, H1, ADD, MUL)
-            o(stt, G3, t["to"], -1.0, G3, ADD, MUL)
-            dtc = tps.tile([P, J, P], F32, name="ps", tag="ps")
-            back = tps.tile([P, J, P], F32, name="ps", tag="ps")
-            o(flip, dtc, [P1, NT, P2, G3])
-            o(final, n, 3, t["qto"], -1.0 / 12.0, X)
-            o(stt, t["ich"], t["ig"], -1.0, t["ich"], ADD, MUL)
-            o(stt, D1, t["t2"], -1.0, dtc, ADD, MUL)
-            o(flip, back, [D1])
-            o(stt, t["fc"], t["fg"], -1.0, t["fc"], ADD, MUL)
-
-            def qn(j):
-                nc.vector.scalar_tensor_tensor(
-                    out=P1[:, j, :], in0=back[:, j, :], scalar=mcol(msq6, g, j), in1=t["mg1"][:, j, :],
-                    op0=MUL, op1=SUB)
-
-            o(stt, t["chq"], t["chq"], -1.0, t["ig"], ADD, MUL)
-            for j in range(J):
-                o(qn, j)
-            o(lambda: nc.vector.tensor_tensor(out=unit_out(n, 4), in0=P1[:], in1=t["ich"][:], op=MUL))
-            o(lambda: nc.vector.tensor_tensor(out=unit_out(n, 5), in0=P1[:], in1=t["fc"][:], op=MUL))
-            o(lambda: nc.vector.tensor_tensor(out=unit_out(n, 6), in0=P1[:], in1=t["chq"][:], op=MUL))
-            return ops
-
-        tok = {}
-        feat = {}
-
-        def quad_spread(g, q):
-            dz = quad_tiles[g, q]
-            inter = dzp.tile([P, 4 * W, J], BF16, name="inter", tag="inter", align_bytes=64)
-            nc.scalar.copy(inter[:], dz[:].rearrange("p j k w -> p (k w) j"))
-            words = dz[:].rearrange("p j k w -> p (j k w)").bitcast(F32)
-            fz = dzp.tile([P, 4 * P, J], BF16, name="fz", tag="fz", align_bytes=64)
-            fw = fz[:].rearrange("p n t -> p (n t)").bitcast(F32).rearrange("p (h a n u) -> p h a n u", h=2, a=2, u=2)
-            for h in range(2):
-                ps = tps.tile([P, 2, 2, P], F32, name="ps", tag="ps")
-                for a in range(2):
-                    for u in range(2):
-                        lo = 256 * (2 * h + a)
-                        nc.tensor.transpose(ps[:, a, u, :], words[:, lo + u : lo + 256 : 2], ident[:])
-                nc.scalar.copy(fw[:, h], ps[:].rearrange("p a u n -> p a n u"))
-            return inter, fz
-
-        def quad_quantize(g, q, inter, fz):
-            tc_ = keep.tile([P, 4 * W], U32, name="tokc%d" % q, tag="tokc%d_%d" % (g, q) if g == 0 else "tokc1_%d" % (q % 2), align_bytes=64)
-            ts_ = keep.tile([P, 4 * W], U8, name="toks%d" % q, tag="toks%d_%d" % (g, q) if g == 0 else "toks1_%d" % (q % 2), align_bytes=64)
-            fc_ = keep.tile([P, 4 * P], U32, name="featc%d" % q, tag="featc%d" % q, align_bytes=64)
-            fs_ = keep.tile([P, 4 * P], U8, name="feats%d" % q, tag="feats%d" % q, align_bytes=64)
+        def quad_tokens(g, q):
+            nm = "%d_%d" % (g, q) if g == 0 else "1_%d" % (q % 3)
+            tc_ = keep.tile([P, 4 * W], U32, name="tokc", tag="tokc" + nm, align_bytes=64)
+            ts_ = keep.tile([P, 4 * W], U8, name="toks", tag="toks" + nm, align_bytes=64)
             tok[g, q] = (tc_, ts_)
+            nc.vector.quantize_mx(
+                out=tc_[:].bitcast(E5M2), scales=ts_[:],
+                in_=quad_tiles[g, q][:].rearrange("p k w j -> p (k w j)"))
+            if g == 1:
+                for kk in range(4):
+                    queues["x"].append(lambda kk=kk: weight_grad(q, kk))
+
+        def quad_features(g, q, fz):
+            fc_ = keep.tile([P, 4 * P], U32, name="featc", tag="featc%d" % q, align_bytes=64)
+            fs_ = keep.tile([P, 4 * P], U8, name="feats", tag="feats%d" % q, align_bytes=64)
             feat[g, q] = (fc_, fs_)
-            return [
-                lambda: nc.vector.quantize_mx(
-                    out=tc_[:].bitcast(E5M2), scales=ts_[:], in_=inter[:].rearrange("p w j -> p (w j)")),
-                lambda: nc.vector.quantize_mx(
-                    out=fc_[:].bitcast(E5M2), scales=fs_[:], in_=fz[:].rearrange("p n t -> p (n t)")),
-            ]
+            nc.vector.quantize_mx(
+                out=fc_[:].bitcast(E5M2), scales=fs_[:], in_=fz[:].rearrange("p j n t -> p (j n t)"))
+            if q == QUADS - 1:
+                for j in range(J):
+                    queues["x"].append(lambda j=j: data_grad(g, j))
 
-        def quad_weight_grad(q):
-            for kk in range(4):
-                unit = 4 * q + kk
-                c, u = divmod(unit, GATES)
-                row = DH * ORDER[u] + W * c
-                acc = mps.tile([P, 512], F32, name="acc", tag="acc")
-                for g in range(GROUPS):
-                    codes, scales = tok[g, q]
-                    nc.tensor.matmul_mx(
-                        out=acc[:],
-                        lhsT=codes[:, W * kk : W * (kk + 1)].bitcast(E5M2),
-                        lhsT_scale=scales[:, W * kk : W * (kk + 1)],
-                        rhs=x_codes[:, DI * g : DI * g + 512].bitcast(E4M3),
-                        rhs_scale=x_scales[:, DI * g : DI * g + 512],
-                        start=(g == 0), stop=(g == GROUPS - 1),
-                    )
-                res = stage.tile([P, DI], F32, name="res", tag="res", bufs=4)
-                nc.scalar.copy(res[:], acc[:, :DI])
-                nc.sync.dma_start(out=out_1[row : row + W, :], in_=res[:])
+        def evacuate(acc, dst):
+            res = stage.tile([P, DI], F32, name="res", tag="res", bufs=3)
+            nc.scalar.copy(res[:], acc[:, :DI])
+            nc.sync.dma_start(out=dst, in_=res[:])
 
-        def data_grad(g):
+        def weight_grad(q, kk):
+            c, u = divmod(4 * q + kk, GATES)
+            row = DH * ORDER[u] + W * c
+            acc = mps.tile([P, 512], F32, name="mb", tag="mb")
+            for g in range(GROUPS):
+                codes, scales = tok[g, q]
+                nc.tensor.matmul_mx(
+                    out=acc[:],
+                    lhsT=codes[:, W * kk : W * (kk + 1)].bitcast(E5M2),
+                    lhsT_scale=scales[:, W * kk : W * (kk + 1)],
+                    rhs=x_codes[:, DI * g : DI * g + 512].bitcast(E4M3),
+                    rhs_scale=x_scales[:, DI * g : DI * g + 512],
+                    start=(g == 0), stop=(g == GROUPS - 1),
+                )
+            evacuate(acc, out_1[row : row + W, :])
+
+        def data_grad(g, j):
             rows = out_0[512 * g : 512 * (g + 1), :].rearrange("(p j) d -> p j d", j=J)
-            for j in range(J):
-                acc = mps.tile([P, 512], F32, name="acc", tag="acc")
-                for q in range(QUADS):
-                    codes, scales = feat[g, q]
-                    nc.tensor.matmul_mx(
-                        out=acc[:],
-                        lhsT=codes[:, P * j : P * (j + 1)].bitcast(E5M2),
-                        lhsT_scale=scales[:, P * j : P * (j + 1)],
-                        rhs=w_codes[:, DI * q : DI * q + 512].bitcast(E4M3),
-                        rhs_scale=w_scales[:, DI * q : DI * q + 512],
-                        start=(q == 0), stop=(q == QUADS - 1),
-                    )
-                res = stage.tile([P, DI], F32, name="res", tag="res", bufs=4)
-                nc.scalar.copy(res[:], acc[:, :DI])
-                nc.sync.dma_start(out=rows[:, j, :], in_=res[:])
+            acc = mps.tile([P, 512], F32, name="mb", tag="mb")
+            for q in range(QUADS):
+                codes, scales = feat[g, q]
+                nc.tensor.matmul_mx(
+                    out=acc[:],
+                    lhsT=codes[:, P * j : P * (j + 1)].bitcast(E5M2),
+                    lhsT_scale=scales[:, P * j : P * (j + 1)],
+                    rhs=w_codes[:, DI * q : DI * q + 512].bitcast(E4M3),
+                    rhs_scale=w_scales[:, DI * q : DI * q + 512],
+                    start=(q == 0), stop=(q == QUADS - 1),
+                )
+            evacuate(acc, rows[:, j, :])
 
-        def load_w(q):
-            wr = stage.tile([P, J, DI], BF16, name="wr", tag="wr")
-            for kk in range(4):
-                c, u = divmod(4 * q + kk, GATES)
-                row = DH * ORDER[u] + W * c
-                nc.sync.dma_start(
-                    out=wr[32 * kk : 32 * (kk + 1), :, :],
-                    in_=weight_ih[row : row + W, :].rearrange("(r j) d -> r j d", j=J))
-            return wr
+        queues = {"half": [], "tq": [], "fq": [], "x": [], "grp": [], "wq": []}
 
-        def load_x(g):
-            xr = stage.tile([P, J, DI], BF16, name="wr", tag="wr")
-            nc.sync.dma_start(out=xr[:], in_=tokens(x, g, 0, DI))
-            return xr
-
-        def group4(src):
-            grp = stage.tile([P, DI, J], BF16, name="grp", tag="grp", align_bytes=64)
-            nc.scalar.copy(grp[:], src[:].rearrange("p j d -> p d j"))
-            return grp
-
-        def quant4(grp, codes, scales, col):
-            flat = grp[:].rearrange("p d j -> p (d j)")
-            return [
-                lambda: nc.vector.quantize_mx(
-                    out=codes[:, col : col + 256].bitcast(E4M3), scales=scales[:, col : col + 256], in_=flat[:, :1024]),
-                lambda: nc.vector.quantize_mx(
-                    out=codes[:, col + 256 : col + DI].bitcast(E4M3), scales=scales[:, col + 256 : col + DI],
-                    in_=flat[:, 1024:]),
-            ]
-
-        def quads_done(c):
+        def quads_done(n):
+            c = n % CHUNKS
             return [q for q in range(QUADS) if GATES * c <= 4 * q + 3 < GATES * (c + 1)]
+
+        def queue_quads(n):
+            g, c = divmod(n, CHUNKS)
+            for q in quads_done(n):
+                fz = dzp.tile([P, J, P, 4], BF16, name="fz", tag="fz", bufs=3, align_bytes=64)
+                for h in range(2):
+                    queues["half"].append(lambda q=q, h=h, fz=fz: quad_half(g, q, h, fz))
+                queues["tq"].append(lambda q=q: quad_tokens(g, q))
+                queues["fq"].append(lambda q=q, fz=fz: quad_features(g, q, fz))
+
+        def fetch(dmas):
+            tile = stage.tile([P, J, DI], BF16, name="wr", tag="wr", bufs=2)
+            for lo, hi, src in dmas:
+                nc.sync.dma_start(out=tile[lo:hi, :, :], in_=src)
+            return tile
+
+        def queue_operand(dmas, codes, scales, col):
+            tile = fetch(dmas)
+
+            def group():
+                if operands:
+                    queue_operand(*operands.pop(0))
+                grp = stage.tile([P, DI, J], BF16, name="grp", tag="grp", align_bytes=64)
+                nc.scalar.copy(grp[:], tile[:].rearrange("p j d -> p d j"))
+                flat = grp[:].rearrange("p d j -> p (d j)")
+
+                def quantize():
+                    for lo, hi in ((0, 256), (256, DI)):
+                        nc.vector.quantize_mx(
+                            out=codes[:, col + lo : col + hi].bitcast(E4M3), scales=scales[:, col + lo : col + hi],
+                            in_=flat[:, 4 * lo : 4 * hi])
+
+                queues["wq"].append(quantize)
+
+            queues["grp"].append(group)
+
+        def unit_rows(q, kk):
+            c, u = divmod(4 * q + kk, GATES)
+            row = DH * ORDER[u] + W * c
+            return weight_ih[row : row + W, :].rearrange("(r j) d -> r j d", j=J)
+
+        operands = [([(0, P, tokens(x, g, 0, DI))], x_codes, x_scales, DI * g) for g in range(GROUPS)]
+        operands += [
+            ([(32 * kk, 32 * kk + 32, unit_rows(q, kk)) for kk in range(4)], w_codes, w_scales, DI * q)
+            for q in range(QUADS)
+        ]
+
+        def v_fc(n):
+            t = st[n]
+            fc = new(n, "fc", act)
+            per_j(lambda j: nc.vector.scalar_tensor_tensor(
+                out=fc[:, j, :], in0=t["fg"][:, j, :], scalar=mcol(m32, n // CHUNKS, j), in1=t["cm"][:, j, :],
+                op0=MUL, op1=MUL))
+
+        def v_q(n):
+            t = st[n]
+            qn = new(n, "qn", vec)
+            per_j(lambda j: nc.vector.scalar_tensor_tensor(
+                out=qn[:, j, :], in0=t["back"][:, j, :], scalar=mcol(m6, n // CHUNKS, j), in1=t["g1"][:, j, :],
+                op0=MUL, op1=SUB))
+
+        def v(nm, a, s, b, op0, op1):
+            def step(n):
+                stt(new(n, nm, vec), st[n][a], s, st[n][b], op0, op1)
+            return step
+
+        def last_final(n):
+            final2(n, 6, st[n]["qn"], st[n]["chq"])
+            queue_quads(n)
+
+        steps = {
+            "sfwd": s_forward,
+            "chq": s_chq,
+            "gb2": lambda n: s_gate(n, "tb2"),
+            "gb1": lambda n: s_gate(n, "tb1"),
+            "gb0": lambda n: s_gate(n, "tb0"),
+            "gto": lambda n: s_gate(n, "to"),
+            "tanh": lambda n: nc.scalar.activation(new(n, "tt", act)[:], st[n]["zf"][:], TANH),
+            "t2": lambda n: nc.scalar.activation(st[n]["tt"][:], st[n]["tt"][:], SQUARE),
+            "load": load,
+            "fgA": lambda n: flip_pair(n, "g4", "g0"),
+            "fgB": lambda n: flip_pair(n, "g3", "g2"),
+            "Fz": lambda n: flip(n, "zf", "ich", "fc"),
+            "Fb2": lambda n: flip(n, "b2", "D2"),
+            "Fb1": lambda n: flip(n, "b1", "D1"),
+            "Fb0": lambda n: flip(n, "b0", "D0"),
+            "Fh1": lambda n: flip(n, "h1", "H1"),
+            "Fh0": lambda n: flip(n, "h0", "E0", "M", "U"),
+            "Fy": lambda n: flip(n, "y", "E0", "M", "U", "H1", "G"),
+            "Fdo": lambda n: flip(n, "do", "NG", "D0", "D1"),
+            "Fdtc": lambda n: flip(n, "dtc", "P0", "P1", "P2", "PO"),
+            "Fback": lambda n: flip(n, "back", "bk"),
+            "ich": lambda n: mul(new(n, "ich", act), st[n]["im"], st[n]["ch"]),
+            "fc": v_fc,
+            "fi": lambda n: stt(st[n]["ich"], st[n]["ig"], -1.0, st[n]["ich"], ADD, MUL),
+            "ff": lambda n: stt(st[n]["fc"], st[n]["fg"], -1.0, st[n]["fc"], ADD, MUL),
+            "fcg": lambda n: stt(st[n]["chq"], st[n]["chq"], -1.0, st[n]["im"], ADD, MUL),
+            "tau": lambda n: mul(new(n, "tau", vec), st[n]["tt"], m_bc[:, n // CHUNKS]),
+            "D2": v("D2", "g4f", -0.5, "tau", MUL, MUL),
+            "G": v("G", "g0s", -3.0, "g4f", MUL, ADD),
+            "E1": v("E1", "g3f", 1.5, "D2", MUL, ADD),
+            "D1": v("D1", "E1", -1.0, "tau", MUL, MUL),
+            "U": v("U", "D2", -1.0, "tau", MUL, MUL),
+            "H1": lambda n: mul(new(n, "H1", vec), st[n]["E1"], st[n]["D2"], ADD),
+            "M": v("M", "D2", 4.0, "D1", MUL, ADD),
+            "NG": v("NG", "G", -1.0, "tau", MUL, MUL),
+            "E0": v("E0", "g2f", 3.0, "M", MUL, ADD),
+            "D0": v("D0", "E0", -1.0, "tau", MUL, MUL),
+            "P0": v("P0", "tb0", 3.0, "h0", ADD, MUL),
+            "P1": v("P1", "tb1", 5.0, "h1", ADD, MUL),
+            "P2": v("P2", "tb2", 7.0, "g4", ADD, MUL),
+            "PO": v("PO", "to", -1.0, "y", ADD, MUL),
+            "bk": v("bk", "tt", -1.0, "dtc", ADD, MUL),
+            "q": v_q,
+            "b2": lambda n: final(n, 0, st[n]["qtb2"], -1.0 / 6.0, st[n]["b2"]),
+            "b1": lambda n: final(n, 1, st[n]["qtb1"], -1.0 / 12.0, st[n]["b1"]),
+            "b0": lambda n: final(n, 2, st[n]["qtb0"], -1.0 / 12.0, st[n]["b0"]),
+            "fo": lambda n: final2(n, 3, st[n]["qto"], st[n]["do"]),
+            "di": lambda n: final2(n, 4, st[n]["qn"], st[n]["ich"]),
+            "df": lambda n: final2(n, 5, st[n]["qn"], st[n]["fc"]),
+            "dc": last_final,
+        }
+
+        def run(queue):
+            if queues[queue]:
+                queues[queue].pop(0)()
 
         with tc.manual_schedule():
             nc.sync.dma_start(out=m_raw[:], in_=mask.rearrange("(g p j) -> p g j", g=GROUPS, j=J))
-            load(0)
+            m_row = stage.tile([P, B], BF16, name="wr", tag="wr", bufs=2)
+            nc.sync.dma_start(out=m_row[:], in_=mask.partition_broadcast(P))
             nc.vector.tensor_copy(out=m32[:], in_=m_raw[:].rearrange("p g j -> p (g j)"))
-            nc.vector.scalar_tensor_tensor(out=msq6[:], in0=m32[:], scalar=1.0 / 6.0, in1=m32[:], op0=MUL, op1=MUL)
-            load(1)
-            s_forward(0)
-            for f in v_forward(0):
-                f()
-            s_gates(0)
-            s_tanh(0)
-
-            operands = [("x", 0), ("x", 1)] + [("w", q) for q in range(QUADS)]
-            pending = []
-            for n in range(GROUPS * CHUNKS):
-                g, c = divmod(n, CHUNKS)
-                last = n == GROUPS * CHUNKS - 1
-                if n + 2 < GROUPS * CHUNKS:
-                    load(n + 2)
-                if not last:
-                    s_forward(n + 1)
-                ops = v_main(n)
-                fwd = [] if last else v_forward(n + 1)
-                small = []
-                if g == 0:
-                    take = 3 if c < 3 else 0
-                    for _ in range(take):
-                        kind, i = operands.pop(0)
-                        if kind == "x":
-                            small += quant4(group4(load_x(i)), x_codes, x_scales, DI * i)
-                        else:
-                            small += quant4(group4(load_w(i)), w_codes, w_scales, DI * i)
-                extra = {}
-                for i, f in enumerate(pending):
-                    extra.setdefault(4 + 3 * i, []).append(f)
-                for i, f in enumerate(fwd):
-                    extra.setdefault(12 + 2 * i, []).append(f)
-                for i, f in enumerate(small):
-                    extra.setdefault(19 + 2 * i, []).append(f)
-                for i, f in enumerate(ops):
-                    f()
-                    for e in extra.get(i, []):
-                        e()
-                    if i == 16 and not last:
-                        s_gates(n + 1)
-                        s_tanh(n + 1)
-                if g == 1 and c == 0:
-                    data_grad(0)
-                if g == 1 and c >= 1:
-                    for q in quads_done(c - 1):
-                        quad_weight_grad(q)
-                pending = []
-                for q in quads_done(c):
-                    inter, fz = quad_spread(g, q)
-                    pending += quad_quantize(g, q, inter, fz)
-                if last:
-                    for f in pending:
-                        f()
-                    for q in quads_done(c):
-                        quad_weight_grad(q)
-                    data_grad(1)
+            nc.vector.tensor_scalar(out=m6[:], in0=m32[:], scalar1=1.0 / 6.0, scalar2=None, op0=MUL)
+            nc.gpsimd.tensor_copy(out=m_bc[:], in_=m_row[:].rearrange("q (g p j) -> q g j p", g=GROUPS, j=J))
+            for n in range(-2, N + 1):
+                if n == 0:
+                    queue_operand(*operands.pop(0))
+                for nm, d in PERIOD:
+                    if nm in queues:
+                        if n >= 0:
+                            run(nm)
+                    elif 0 <= n + d < N:
+                        steps[nm](n + d)
+            for nm in ("half", "half", "half", "half", "tq", "x", "x", "x", "x", "tq", "x", "x", "x", "x", "fq", "fq"):
+                run(nm)
+            while queues["x"]:
+                run("x")

@@ -38,15 +38,18 @@ K6 = (1.0 / 6.0) ** 0.5
 K12 = (1.0 / 12.0) ** 0.5
 N = GROUPS * CHUNKS
 PERIOD = [
-    ("Fdtc", -1), ("fq", 0), ("fcg", 0), ("gb2", 0), ("fgB", 0), ("D2", 0), ("bk", -1), ("x", 0), ("E1", 0), ("x", 0),
-    ("gto", 0), ("U", 0), ("D1", 0), ("Fb2", 0), ("b2", 0), ("sfwd", 1), ("x", 0), ("M", 0), ("Fback", -1), ("Fb1", 0),
-    ("H1", 0), ("E0", 0), ("x", 0), ("x", 0), ("G", 0), ("grp", 0), ("Fh1", 0), ("q", -1), ("b1", 0), ("df", -1),
-    ("P1", 0), ("di", -1), ("x", 0), ("tq", 0), ("dc", -1), ("gb1", 1), ("NG", 0), ("half", 0), ("gb0", 1), ("Fh0", 0),
-    ("fgA", 1), ("load", 2), ("Fy", 0), ("half", 0), ("wq", 0), ("t2", 0), ("D0", 0), ("fc", 1), ("ich", 1), ("half", 0),
-    ("Fb0", 0), ("P0", 0), ("Fdo", 0), ("Fz", 1), ("PO", 0), ("tanh", 1), ("x", 0), ("P2", 0), ("tq", 0), ("b0", 0),
-    ("fq", 0), ("tq", 0), ("wq", 0), ("fo", 0), ("x", 0), ("chq", 1), ("fi", 1), ("ff", 1), ("x", 0), ("tau", 1),
-    ("half", 0), ("grp", 0),
+    ("tau", 0), ("ldB", 1), ("ldD", 1), ("gb2", 0), ("fi", 0), ("grp", 0), ("grp", 0), ("D2", 0), ("G", 0), ("E1", 0),
+    ("half", 0), ("x", 0), ("chq", 0), ("wq", 0), ("gto", 0), ("Fdtc", -1), ("gb0", 0), ("fq", 0), ("x", 0), ("x", 0),
+    ("qb2", 0), ("D1", 0), ("tq", 0), ("gi", 1), ("x", 0), ("grp", 0), ("gch", 1), ("U", 0), ("bk", -1), ("Fback", -1),
+    ("qo", 0), ("Fb2", 0), ("im", 1), ("M", 0), ("x", 0), ("fo", -1), ("half", 0), ("H1", 0), ("qb0", 0), ("E0", 0),
+    ("NG", 0), ("q", -1), ("fcg", 0), ("Fh1", 0), ("df", -1), ("di", -1), ("gf", 1), ("b2", 0), ("P2", 0), ("Fb1", 0),
+    ("dc", -1), ("x", 0), ("x", 0), ("x", 0), ("ldA", 2), ("P1", 0), ("ldC", 1), ("tq", 0), ("Fh0", 0), ("fgA", 1),
+    ("half", 0), ("gb1", 1), ("ich", 1), ("b1", 0), ("fc", 1), ("D0", 0), ("Fy", 0), ("x", 0), ("P0", 0), ("fq", 0),
+    ("qb1", 1), ("x", 0), ("Fz", 1), ("tanh", 1), ("Fb0", 0), ("tq", 0), ("t2", 0), ("PO", 0), ("wq", 0), ("ff", 1),
+    ("wq", 0), ("half", 0), ("fgB", 1), ("b0", 0), ("Fdo", 0),
 ]
+HEAD = ["ldA", "gi", "ldB", "im", "gf", "gch", "fgA", "fc", "ich", "ldC", "gb2", "qb2", "chq", "Fz", "tau", "tanh", "gb1", "gto", "ff", "fgB", "fi", "qb1", "gb0", "ldD", "qo", "fcg", "qb0", "t2"]
+TAIL = ["e1", "x", "fq", "tq", "x", "e2", "d2", "x", "x", "e0", "d0", "x", "d1", "half", "x", "x", "x", "half", "e3", "d3"]
 
 
 def tile_share_lstm_cell_pa_v_kernel(
@@ -57,11 +60,11 @@ def tile_share_lstm_cell_pa_v_kernel(
     nc = tc.nc
     with ExitStack() as ctx:
         keep = ctx.enter_context(tc.tile_pool(name="keep", bufs=1))
-        raw = ctx.enter_context(tc.tile_pool(name="raw", bufs=3))
+        raw = ctx.enter_context(tc.tile_pool(name="raw", bufs=2))
         act = ctx.enter_context(tc.tile_pool(name="act", bufs=2))
         vec = ctx.enter_context(tc.tile_pool(name="vec", bufs=1))
         dzp = ctx.enter_context(tc.tile_pool(name="dzp", bufs=2))
-        stage = ctx.enter_context(tc.tile_pool(name="stage", bufs=2))
+        stage = ctx.enter_context(tc.tile_pool(name="stage", bufs=1))
         gps = ctx.enter_context(tc.psum_pool(name="gps", bufs=2))
         fps = ctx.enter_context(tc.psum_pool(name="fps", bufs=4))
         mps = ctx.enter_context(tc.psum_pool(name="mps", bufs=2))
@@ -90,26 +93,39 @@ def tile_share_lstm_cell_pa_v_kernel(
         def mcol(tile, g, j):
             return tile[:, g * J + j : g * J + j + 1]
 
-        st = {}
+        st = {n: {} for n in range(N)}
 
         def tokens(src, g, col0, width):
             return src[512 * g : 512 * (g + 1), col0 : col0 + width].rearrange("(p j) w -> p j w", j=J)
 
-        LOADS = (
-            ("ig", pre, 0, F32), ("ch", pre, 3 * DH, F32), ("fg", pre, DH, F32), ("cm", c_minors, 0, BF16),
-            ("g4", grad_4, 0, BF16), ("g0", grad_0, 0, BF16), ("g3", grad_3, 0, BF16), ("g2", grad_2, 0, BF16),
-            ("tb2", pre_s, 2 * DH, F32), ("tb1", pre_s, DH, F32), ("tb0", pre_s, 0, F32),
-            ("to", pre, 2 * DH, F32), ("g1", grad_1, 0, BF16),
-        )
+        LOADS = {
+            "ldA": (("ig", pre, 0, F32), ("ch", pre, 3 * DH, F32), ("fg", pre, DH, F32), ("cm", c_minors, 0, BF16)),
+            "ldB": (("g4", grad_4, 0, BF16), ("g0", grad_0, 0, BF16), ("g3", grad_3, 0, BF16), ("g2", grad_2, 0, BF16)),
+            "ldC": (("tb1", pre_s, DH, F32), ("tb0", pre_s, 0, F32), ("tb2", pre_s, 2 * DH, F32),
+                    ("to", pre, 2 * DH, F32)),
+            "ldD": (("g1", grad_1, 0, BF16),),
+        }
 
-        def load(n):
-            g, c = divmod(n, CHUNKS)
-            t = {}
-            for nm, src, col, dt in LOADS:
-                tl = raw.tile([P, J, W], dt, name=nm, tag=nm, bufs=2 if nm in ("cm", "g0", "g3", "g2") else 3)
-                nc.sync.dma_start(out=tl[:], in_=tokens(src, g, col + c * W, W))
-                t[nm] = tl
-            st[n] = t
+        def load(part):
+            def step(n):
+                if n % 2:
+                    return
+                g, c = divmod(n, CHUNKS)
+                tiles = [(nm, src, col, raw.tile([P, J, 2 * W], dt, name=nm, tag=nm)) for nm, src, col, dt in LOADS[part]]
+                for nm, src, col, tl in tiles:
+                    st[n][nm] = tl[:, :, :W]
+                    st[n + 1][nm] = tl[:, :, W:]
+                    if n:
+                        nc.sync.dma_start(out=tl[:], in_=tokens(src, g, col + c * W, 2 * W))
+                    else:
+                        nc.sync.dma_start(out=st[0][nm], in_=tokens(src, 0, col, W))
+                if n == 0:
+                    for nm, src, col, tl in tiles:
+                        late.append(lambda nm=nm, src=src, col=col: nc.sync.dma_start(
+                            out=st[1][nm], in_=tokens(src, 0, col + W, W)))
+            return step
+
+        late = []
 
         def new(n, nm, pool, dt=F32):
             tl = pool.tile([P, J, W], dt, name=nm, tag=nm)
@@ -135,26 +151,22 @@ def tile_share_lstm_cell_pa_v_kernel(
             for j in range(J):
                 fn(j)
 
-        def s_forward(n):
+        def s_im(n):
             t = st[n]
-            g = n // CHUNKS
             im = new(n, "im", act)
-            nc.scalar.activation(t["ig"][:], t["ig"][:], SIGMOID)
-            for j in range(J):
-                nc.scalar.activation(im[:, j, :], t["ig"][:, j, :], COPY, scale=mcol(m32, g, j))
-            nc.scalar.activation(t["ch"][:], t["ch"][:], TANH)
-            nc.scalar.activation(t["fg"][:], t["fg"][:], SIGMOID)
+            per_j(lambda j: nc.scalar.activation(
+                im[:, j, :], t["ig"][:, j, :], COPY, scale=mcol(m32, n // CHUNKS, j)))
 
-        def s_chq(n):
-            nc.scalar.activation(new(n, "chq", act)[:], st[n]["ch"][:], SQUARE)
+        def s_gate(nm, fn, scale=1.0):
+            return lambda n: nc.scalar.activation(st[n][nm], st[n][nm], fn, scale=scale)
 
-        def s_gate(n, nm):
-            t = st[n]
-            nc.scalar.activation(t[nm][:], t[nm][:], TANH, scale=-0.5 if nm == "to" else 0.5)
-            sq = new(n, "q" + nm, act)
-            nc.scalar.activation(sq[:], t[nm][:], SQUARE, scale=K6 if nm == "tb2" else K12)
-            if nm == "to":
-                nc.scalar.activation(sq[:], sq[:], COPY, scale=-1.0, bias=1.0 / 12.0)
+        def s_square(nm, scale):
+            return lambda n: nc.scalar.activation(new(n, "q" + nm, act)[:], st[n][nm], SQUARE, scale=scale)
+
+        def s_oq(n):
+            sq = new(n, "qto", act)
+            nc.scalar.activation(sq[:], st[n]["to"], SQUARE, scale=K12)
+            nc.scalar.activation(sq[:], sq[:], COPY, scale=-1.0, bias=1.0 / 12.0)
 
         def flip_pair(n, a, b):
             t = st[n]
@@ -167,15 +179,26 @@ def tile_share_lstm_cell_pa_v_kernel(
                 nc.scalar.copy(new(n, "g0s", act, BF16)[:], t["g0f"])
 
         quad_tiles = {}
+        halves = []
         tok = {}
         feat = {}
+
+        left = {}
 
         def unit_out(n, u):
             g, c = divmod(n, CHUNKS)
             q, kk = divmod(GATES * c + u, 4)
             if (g, q) not in quad_tiles:
-                quad_tiles[g, q] = dzp.tile([P, 4, W, J], BF16, name="dz", tag="dz", bufs=4, align_bytes=64)
+                quad_tiles[g, q] = dzp.tile([P, 4, W, J], BF16, name="dz", tag="dz", bufs=3, align_bytes=64)
+                left[g, q] = 4
             return quad_tiles[g, q][:, kk, :, :]
+
+        def unit_done(n, u):
+            g, c = divmod(n, CHUNKS)
+            q = (GATES * c + u) // 4
+            left[g, q] -= 1
+            if left[g, q] == 0:
+                queue_quad(g, q)
 
         def inter(tile):
             return tile[:].rearrange("p j w -> p w j")
@@ -183,9 +206,17 @@ def tile_share_lstm_cell_pa_v_kernel(
         def final(n, u, sq, cst, val):
             nc.vector.scalar_tensor_tensor(
                 out=unit_out(n, u), in0=inter(sq), scalar=cst, in1=inter(val), op0=ADD, op1=MUL)
+            unit_done(n, u)
 
         def final2(n, u, a, b):
             nc.vector.tensor_tensor(out=unit_out(n, u), in0=inter(a), in1=inter(b), op=MUL)
+            unit_done(n, u)
+
+        ending = [False]
+        stores = []
+
+        def copier(i):
+            return nc.vector.tensor_copy if ending[0] and i % 2 else nc.scalar.copy
 
         def quad_half(g, q, h, fz):
             words = quad_tiles[g, q][:].rearrange("p k w j -> p (k w j)").bitcast(F32)
@@ -193,10 +224,11 @@ def tile_share_lstm_cell_pa_v_kernel(
             for t in range(4):
                 nc.tensor.transpose(ps[:, t, :], words[:, 2 * t + h :: 8], ident[:])
             src = ps[:].rearrange("p t n -> p (t n)").bitcast(BF16).rearrange("p (t n e) -> p e n t", t=4, e=2)
-            nc.scalar.copy(fz[:, 2 * h : 2 * h + 2, :, :], src)
+            copier(h)(fz[:, 2 * h : 2 * h + 2, :, :], src)
+            halves.append((g, q))
 
         def quad_tokens(g, q):
-            nm = "%d_%d" % (g, q) if g == 0 else "1_%d" % (q % 3)
+            nm = "%d_%d" % (g, q) if g == 0 else "1_%d" % (q % 2)
             tc_ = keep.tile([P, 4 * W], U32, name="tokc", tag="tokc" + nm, align_bytes=64)
             ts_ = keep.tile([P, 4 * W], U8, name="toks", tag="toks" + nm, align_bytes=64)
             tok[g, q] = (tc_, ts_)
@@ -213,14 +245,16 @@ def tile_share_lstm_cell_pa_v_kernel(
             feat[g, q] = (fc_, fs_)
             nc.vector.quantize_mx(
                 out=fc_[:].bitcast(E5M2), scales=fs_[:], in_=fz[:].rearrange("p j n t -> p (j n t)"))
-            if q == QUADS - 1:
-                for j in range(J):
-                    queues["x"].append(lambda j=j: data_grad(g, j))
+            if q == QUADS - 1 and g == 0:
+                queues["x"][:0] = [lambda j=j: data_grad(0, j) for j in range(J)]
 
-        def evacuate(acc, dst):
-            res = stage.tile([P, DI], F32, name="res", tag="res", bufs=3)
-            nc.scalar.copy(res[:], acc[:, :DI])
-            nc.sync.dma_start(out=dst, in_=res[:])
+        def evacuate(acc, dst, i):
+            res = stage.tile([P, DI], F32, name="res", tag="res", bufs=4)
+            copier(i)(res[:], acc[:, :DI])
+            if ending[0]:
+                nc.sync.dma_start(out=dst, in_=res[:])
+            else:
+                stores.append(lambda: nc.scalar.dma_start(out=dst, in_=res[:]))
 
         def weight_grad(q, kk):
             c, u = divmod(4 * q + kk, GATES)
@@ -236,12 +270,16 @@ def tile_share_lstm_cell_pa_v_kernel(
                     rhs_scale=x_scales[:, DI * g : DI * g + 512],
                     start=(g == 0), stop=(g == GROUPS - 1),
                 )
-            evacuate(acc, out_1[row : row + W, :])
+            evacuate(acc, out_1[row : row + W, :], kk)
 
-        def data_grad(g, j):
-            rows = out_0[512 * g : 512 * (g + 1), :].rearrange("(p j) d -> p j d", j=J)
-            acc = mps.tile([P, 512], F32, name="mb", tag="mb")
-            for q in range(QUADS):
+        accs = {}
+
+        def data_grad(g, j, lo=0, hi=QUADS):
+            if lo == 0:
+                pool, tag = (fps, "flipped") if hi < QUADS else (mps, "mb")
+                accs[g, j] = pool.tile([P, 512], F32, name=tag, tag=tag)
+            acc = accs[g, j]
+            for q in range(lo, hi):
                 codes, scales = feat[g, q]
                 nc.tensor.matmul_mx(
                     out=acc[:],
@@ -251,27 +289,23 @@ def tile_share_lstm_cell_pa_v_kernel(
                     rhs_scale=w_scales[:, DI * q : DI * q + 512],
                     start=(q == 0), stop=(q == QUADS - 1),
                 )
-            evacuate(acc, rows[:, j, :])
+            if hi == QUADS:
+                rows = out_0[512 * g : 512 * (g + 1), :].rearrange("(p j) d -> p j d", j=J)
+                evacuate(acc, rows[:, j, :], j)
 
         queues = {"half": [], "tq": [], "fq": [], "x": [], "grp": [], "wq": []}
 
-        def quads_done(n):
-            c = n % CHUNKS
-            return [q for q in range(QUADS) if GATES * c <= 4 * q + 3 < GATES * (c + 1)]
-
-        def queue_quads(n):
-            g, c = divmod(n, CHUNKS)
-            for q in quads_done(n):
-                fz = dzp.tile([P, J, P, 4], BF16, name="fz", tag="fz", bufs=3, align_bytes=64)
-                for h in range(2):
-                    queues["half"].append(lambda q=q, h=h, fz=fz: quad_half(g, q, h, fz))
-                queues["tq"].append(lambda q=q: quad_tokens(g, q))
-                queues["fq"].append(lambda q=q, fz=fz: quad_features(g, q, fz))
+        def queue_quad(g, q):
+            fz = dzp.tile([P, J, P, 4], BF16, name="fz", tag="fz", bufs=2, align_bytes=64)
+            for h in range(2):
+                queues["half"].append(lambda h=h: quad_half(g, q, h, fz))
+            queues["tq"].append(lambda: quad_tokens(g, q))
+            queues["fq"].append(lambda: quad_features(g, q, fz))
 
         def fetch(dmas):
             tile = stage.tile([P, J, DI], BF16, name="wr", tag="wr", bufs=2)
             for lo, hi, src in dmas:
-                nc.sync.dma_start(out=tile[lo:hi, :, :], in_=src)
+                nc.scalar.dma_start(out=tile[lo:hi, :, :], in_=src)
             return tile
 
         def queue_operand(dmas, codes, scales, col):
@@ -324,20 +358,33 @@ def tile_share_lstm_cell_pa_v_kernel(
                 stt(new(n, nm, vec), st[n][a], s, st[n][b], op0, op1)
             return step
 
-        def last_final(n):
-            final2(n, 6, st[n]["qn"], st[n]["chq"])
-            queue_quads(n)
+
+        def v_over(nm, a, s, b, op0, op1):
+            def step(n):
+                stt(st[n][a], st[n][a], s, st[n][b], op0, op1)
+                st[n][nm] = st[n][a]
+            return step
 
         steps = {
-            "sfwd": s_forward,
-            "chq": s_chq,
-            "gb2": lambda n: s_gate(n, "tb2"),
-            "gb1": lambda n: s_gate(n, "tb1"),
-            "gb0": lambda n: s_gate(n, "tb0"),
-            "gto": lambda n: s_gate(n, "to"),
+            "gi": s_gate("ig", SIGMOID),
+            "im": s_im,
+            "gch": s_gate("ch", TANH),
+            "gf": s_gate("fg", SIGMOID),
+            "chq": s_gate("ch", SQUARE),
+            "gb2": s_gate("tb2", TANH, 0.5),
+            "gb1": s_gate("tb1", TANH, 0.5),
+            "gb0": s_gate("tb0", TANH, 0.5),
+            "gto": s_gate("to", TANH, -0.5),
+            "qb2": s_square("tb2", K6),
+            "qb1": s_square("tb1", K12),
+            "qb0": s_square("tb0", K12),
+            "qo": s_oq,
             "tanh": lambda n: nc.scalar.activation(new(n, "tt", act)[:], st[n]["zf"][:], TANH),
             "t2": lambda n: nc.scalar.activation(st[n]["tt"][:], st[n]["tt"][:], SQUARE),
-            "load": load,
+            "ldA": load("ldA"),
+            "ldB": load("ldB"),
+            "ldC": load("ldC"),
+            "ldD": load("ldD"),
             "fgA": lambda n: flip_pair(n, "g4", "g0"),
             "fgB": lambda n: flip_pair(n, "g3", "g2"),
             "Fz": lambda n: flip(n, "zf", "ich", "fc"),
@@ -354,7 +401,7 @@ def tile_share_lstm_cell_pa_v_kernel(
             "fc": v_fc,
             "fi": lambda n: stt(st[n]["ich"], st[n]["ig"], -1.0, st[n]["ich"], ADD, MUL),
             "ff": lambda n: stt(st[n]["fc"], st[n]["fg"], -1.0, st[n]["fc"], ADD, MUL),
-            "fcg": lambda n: stt(st[n]["chq"], st[n]["chq"], -1.0, st[n]["im"], ADD, MUL),
+            "fcg": lambda n: stt(st[n]["ch"], st[n]["ch"], -1.0, st[n]["im"], ADD, MUL),
             "tau": lambda n: mul(new(n, "tau", vec), st[n]["tt"], m_bc[:, n // CHUNKS]),
             "D2": v("D2", "g4f", -0.5, "tau", MUL, MUL),
             "G": v("G", "g0s", -3.0, "g4f", MUL, ADD),
@@ -366,11 +413,11 @@ def tile_share_lstm_cell_pa_v_kernel(
             "NG": v("NG", "G", -1.0, "tau", MUL, MUL),
             "E0": v("E0", "g2f", 3.0, "M", MUL, ADD),
             "D0": v("D0", "E0", -1.0, "tau", MUL, MUL),
-            "P0": v("P0", "tb0", 3.0, "h0", ADD, MUL),
-            "P1": v("P1", "tb1", 5.0, "h1", ADD, MUL),
-            "P2": v("P2", "tb2", 7.0, "g4", ADD, MUL),
-            "PO": v("PO", "to", -1.0, "y", ADD, MUL),
-            "bk": v("bk", "tt", -1.0, "dtc", ADD, MUL),
+            "P0": v_over("P0", "tb0", 3.0, "h0", ADD, MUL),
+            "P1": v_over("P1", "tb1", 5.0, "h1", ADD, MUL),
+            "P2": v_over("P2", "tb2", 7.0, "g4", ADD, MUL),
+            "PO": v_over("PO", "to", -1.0, "y", ADD, MUL),
+            "bk": v_over("bk", "tt", -1.0, "dtc", ADD, MUL),
             "q": v_q,
             "b2": lambda n: final(n, 0, st[n]["qtb2"], -1.0 / 6.0, st[n]["b2"]),
             "b1": lambda n: final(n, 1, st[n]["qtb1"], -1.0 / 12.0, st[n]["b1"]),
@@ -378,11 +425,15 @@ def tile_share_lstm_cell_pa_v_kernel(
             "fo": lambda n: final2(n, 3, st[n]["qto"], st[n]["do"]),
             "di": lambda n: final2(n, 4, st[n]["qn"], st[n]["ich"]),
             "df": lambda n: final2(n, 5, st[n]["qn"], st[n]["fc"]),
-            "dc": last_final,
+            "dc": lambda n: final2(n, 6, st[n]["qn"], st[n]["ch"]),
         }
 
         def run(queue):
-            if queues[queue]:
+            held = (queue == "grp" and queues["wq"]) or (
+                queue == "fq" and (2 * len(feat) + 2 > len(halves) or len(feat) == QUADS and (0, J - 1) not in accs))
+            if queue == "x" and stores:
+                stores.pop(0)()
+            if queues[queue] and not held:
                 queues[queue].pop(0)()
 
         with tc.manual_schedule():
@@ -392,16 +443,32 @@ def tile_share_lstm_cell_pa_v_kernel(
             nc.vector.tensor_copy(out=m32[:], in_=m_raw[:].rearrange("p g j -> p (g j)"))
             nc.vector.tensor_scalar(out=m6[:], in0=m32[:], scalar1=1.0 / 6.0, scalar2=None, op0=MUL)
             nc.gpsimd.tensor_copy(out=m_bc[:], in_=m_row[:].rearrange("q (g p j) -> q g j p", g=GROUPS, j=J))
-            for n in range(-2, N + 1):
-                if n == 0:
-                    queue_operand(*operands.pop(0))
+            early = [nm for nm, d in PERIOD if d > 0]
+            for nm in HEAD:
+                if nm in early:
+                    steps[nm](0)
+            for fn in late:
+                fn()
+            queue_operand(*operands.pop(0))
+            for nm, d in PERIOD:
+                if d == 2:
+                    steps[nm](1)
+            for n in range(N + 1):
                 for nm, d in PERIOD:
                     if nm in queues:
-                        if n >= 0:
+                        if nm != "grp" or n > 0:
                             run(nm)
                     elif 0 <= n + d < N:
                         steps[nm](n + d)
-            for nm in ("half", "half", "half", "half", "tq", "x", "x", "x", "x", "tq", "x", "x", "x", "x", "fq", "fq"):
-                run(nm)
+            ending[0] = True
+            while stores:
+                stores.pop(0)()
+            for nm in TAIL:
+                if nm[0] == "e":
+                    data_grad(1, int(nm[1]), 0, QUADS - 1)
+                elif nm[0] == "d":
+                    data_grad(1, int(nm[1]), QUADS - 1)
+                else:
+                    run(nm)
             while queues["x"]:
                 run("x")

@@ -37,19 +37,21 @@ ORDER = [6, 5, 4, 2, 0, 1, 3]
 K6 = (1.0 / 6.0) ** 0.5
 K12 = (1.0 / 12.0) ** 0.5
 N = GROUPS * CHUNKS
+DG = 4
+GR_BANKS, FLIP_BANKS, MX_BANKS = 1, 4, 2
 PERIOD = [
-    ("tau", 0), ("ldB", 1), ("ldD", 1), ("gb2", 0), ("fi", 0), ("grp", 0), ("grp", 0), ("D2", 0), ("G", 0), ("E1", 0),
-    ("half", 0), ("x", 0), ("chq", 0), ("wq", 0), ("gto", 0), ("Fdtc", -1), ("gb0", 0), ("fq", 0), ("x", 0), ("x", 0),
-    ("qb2", 0), ("D1", 0), ("tq", 0), ("gi", 1), ("x", 0), ("grp", 0), ("gch", 1), ("U", 0), ("bk", -1), ("Fback", -1),
-    ("qo", 0), ("Fb2", 0), ("im", 1), ("M", 0), ("x", 0), ("fo", -1), ("half", 0), ("H1", 0), ("qb0", 0), ("E0", 0),
-    ("NG", 0), ("q", -1), ("fcg", 0), ("Fh1", 0), ("df", -1), ("di", -1), ("gf", 1), ("b2", 0), ("P2", 0), ("Fb1", 0),
-    ("dc", -1), ("x", 0), ("x", 0), ("x", 0), ("ldA", 2), ("P1", 0), ("ldC", 1), ("tq", 0), ("Fh0", 0), ("fgA", 1),
-    ("half", 0), ("gb1", 1), ("ich", 1), ("b1", 0), ("fc", 1), ("D0", 0), ("Fy", 0), ("x", 0), ("P0", 0), ("fq", 0),
-    ("qb1", 1), ("x", 0), ("Fz", 1), ("tanh", 1), ("Fb0", 0), ("tq", 0), ("t2", 0), ("PO", 0), ("wq", 0), ("ff", 1),
-    ("wq", 0), ("half", 0), ("fgB", 1), ("b0", 0), ("Fdo", 0),
+    ("fcg", -1), ("PO", -1), ("ff", 0), ("half", 0), ("fgB", 0), ("t2", -1), ("grp", 0), ("tau", 0), ("P0", -1), ("x", 0),
+    ("gb1", 0), ("G", 0), ("D2", 0), ("ldD", 1), ("gb0", 0), ("Fdo", -1), ("x", 0), ("b0", -1), ("E1", 0), ("gto", 0),
+    ("qb1", 0), ("Fdtc", -1), ("Fb2", 0), ("ldA", 1), ("x", 0), ("fi", 0), ("tq", 0), ("fq", 0), ("D1", 0), ("tq", 0),
+    ("ldC", 1), ("H1", 0), ("wq", 0), ("qb2", 0), ("x", 0), ("ldB", 1), ("gi", 1), ("fo", -1), ("bk", -1), ("x", 0),
+    ("Fback", -1), ("gf", 1), ("half", 0), ("M", 0), ("Fh1", 0), ("U", 0), ("Fb1", 0), ("E0", 0), ("b2", 0), ("q", -1),
+    ("P2", 0), ("df", -1), ("gch", 1), ("x", 0), ("grp", 0), ("chq", 0), ("im", 1), ("Fh0", 0), ("x", 0), ("di", -1),
+    ("dc", -1), ("qo", 0), ("grp", 0), ("D0", 0), ("half", 0), ("qb0", 0), ("fgA", 1), ("P1", 0), ("x", 0), ("Fy", 0),
+    ("wq", 0), ("tq", 0), ("wq", 0), ("b1", 0), ("ich", 1), ("x", 0), ("fc", 1), ("Fz", 1), ("tanh", 1), ("Fb0", 0),
+    ("early", 0), ("fq", 0), ("x", 0), ("half", 0), ("NG", 0), ("gb2", 1),
 ]
-HEAD = ["ldA", "gi", "ldB", "im", "gf", "gch", "fgA", "fc", "ich", "ldC", "gb2", "qb2", "chq", "Fz", "tau", "tanh", "gb1", "gto", "ff", "fgB", "fi", "qb1", "gb0", "ldD", "qo", "fcg", "qb0", "t2"]
-TAIL = ["e1", "x", "fq", "tq", "x", "e2", "d2", "x", "x", "e0", "d0", "x", "d1", "half", "x", "x", "x", "half", "e3", "d3"]
+HEAD = ["ldA", "ldB", "gi", "ldC", "fgB", "im", "gf", "gto", "fc", "gch", "ich", "gb0", "fgA", "Fz", "ldD", "tanh", "gb2", "qb0", "qb2", "chq", "fcg", "ff", "fi", "qo", "tau", "gb1", "qb1", "t2"]
+TAIL = ["half", "fq", "d3", "x", "e3", "x", "x", "x", "d2", "x", "d0", "x", "half", "x", "tq", "e2", "e1", "x", "d1", "e0"]
 
 
 def tile_share_lstm_cell_pa_v_kernel(
@@ -65,9 +67,10 @@ def tile_share_lstm_cell_pa_v_kernel(
         vec = ctx.enter_context(tc.tile_pool(name="vec", bufs=1))
         dzp = ctx.enter_context(tc.tile_pool(name="dzp", bufs=2))
         stage = ctx.enter_context(tc.tile_pool(name="stage", bufs=1))
-        gps = ctx.enter_context(tc.psum_pool(name="gps", bufs=2))
-        fps = ctx.enter_context(tc.psum_pool(name="fps", bufs=4))
-        mps = ctx.enter_context(tc.psum_pool(name="mps", bufs=2))
+        gps = ctx.enter_context(tc.psum_pool(name="gps", bufs=GR_BANKS))
+        fps = ctx.enter_context(tc.psum_pool(name="fps", bufs=FLIP_BANKS))
+        aps = ctx.enter_context(tc.psum_pool(name="aps", bufs=1))
+        mps = ctx.enter_context(tc.psum_pool(name="mps", bufs=MX_BANKS))
 
         ident = keep.tile([P, P], F32, name="ident")
         make_identity(nc, ident[:])
@@ -176,7 +179,9 @@ def tile_share_lstm_cell_pa_v_kernel(
                     nc.tensor.transpose(bank[:, i, j, :], t[nm][:, j, :], ident_bf[:])
                 t[nm + "f"] = bank[:, i]
             if b == "g0":
-                nc.scalar.copy(new(n, "g0s", act, BF16)[:], t["g0f"])
+                both = act.tile([P, 2, J, W], BF16, name="gs", tag="gs")
+                nc.scalar.copy(both[:], bank[:])
+                t["g4s"], t["g0s"] = both[:, 0], both[:, 1]
 
         quad_tiles = {}
         halves = []
@@ -208,17 +213,26 @@ def tile_share_lstm_cell_pa_v_kernel(
                 out=unit_out(n, u), in0=inter(sq), scalar=cst, in1=inter(val), op0=ADD, op1=MUL)
             unit_done(n, u)
 
+        def runs_of_four(tile):
+            return tile[:].rearrange("p j (c i) -> p c j i", i=4)
+
         def final2(n, u, a, b):
-            nc.vector.tensor_tensor(out=unit_out(n, u), in0=inter(a), in1=inter(b), op=MUL)
+            nc.vector.tensor_tensor(
+                out=unit_out(n, u).rearrange("p (c i) j -> p c j i", i=4),
+                in0=runs_of_four(a), in1=runs_of_four(b), op=MUL)
             unit_done(n, u)
 
         ending = [False]
-        stores = []
 
         def copier(i):
             return nc.vector.tensor_copy if ending[0] and i % 2 else nc.scalar.copy
 
-        def quad_half(g, q, h, fz):
+        fz_tiles = {}
+
+        def quad_half(g, q, h):
+            if h == 0:
+                fz_tiles[g, q] = dzp.tile([P, J, P, 4], BF16, name="fz", tag="fz", bufs=2, align_bytes=64)
+            fz = fz_tiles[g, q]
             words = quad_tiles[g, q][:].rearrange("p k w j -> p (k w j)").bitcast(F32)
             ps = mps.tile([P, 4, P], F32, name="mb", tag="mb")
             for t in range(4):
@@ -237,26 +251,29 @@ def tile_share_lstm_cell_pa_v_kernel(
                 in_=quad_tiles[g, q][:].rearrange("p k w j -> p (k w j)"))
             if g == 1:
                 for kk in range(4):
+                    undone.append(kk)
                     queues["x"].append(lambda kk=kk: weight_grad(q, kk))
 
-        def quad_features(g, q, fz):
+        def quad_features(g, q):
+            fz = fz_tiles[g, q]
             fc_ = keep.tile([P, 4 * P], U32, name="featc", tag="featc%d" % q, align_bytes=64)
             fs_ = keep.tile([P, 4 * P], U8, name="feats", tag="feats%d" % q, align_bytes=64)
             feat[g, q] = (fc_, fs_)
             nc.vector.quantize_mx(
                 out=fc_[:].bitcast(E5M2), scales=fs_[:], in_=fz[:].rearrange("p j n t -> p (j n t)"))
             if q == QUADS - 1 and g == 0:
-                queues["x"][:0] = [lambda j=j: data_grad(0, j) for j in range(J)]
+                queues["x"][:0] = [
+                    lambda j=j, hi=hi: data_grad(0, j, hi) for j in range(J) for hi in (DG, QUADS)]
 
         def evacuate(acc, dst, i):
             res = stage.tile([P, DI], F32, name="res", tag="res", bufs=4)
             copier(i)(res[:], acc[:, :DI])
-            if ending[0]:
-                nc.sync.dma_start(out=dst, in_=res[:])
-            else:
-                stores.append(lambda: nc.scalar.dma_start(out=dst, in_=res[:]))
+            nc.sync.dma_start(out=dst, in_=res[:])
+
+        undone = []
 
         def weight_grad(q, kk):
+            undone.pop()
             c, u = divmod(4 * q + kk, GATES)
             row = DH * ORDER[u] + W * c
             acc = mps.tile([P, 512], F32, name="mb", tag="mb")
@@ -273,10 +290,13 @@ def tile_share_lstm_cell_pa_v_kernel(
             evacuate(acc, out_1[row : row + W, :], kk)
 
         accs = {}
+        reached = {}
+        finished = []
 
-        def data_grad(g, j, lo=0, hi=QUADS):
+        def data_grad(g, j, hi=QUADS):
+            lo = reached.get((g, j), 0)
             if lo == 0:
-                pool, tag = (fps, "flipped") if hi < QUADS else (mps, "mb")
+                pool, tag = (aps, "acc") if g == 0 or j == 0 else (gps, "gb") if j == 1 else (fps, "flipped")
                 accs[g, j] = pool.tile([P, 512], F32, name=tag, tag=tag)
             acc = accs[g, j]
             for q in range(lo, hi):
@@ -289,23 +309,24 @@ def tile_share_lstm_cell_pa_v_kernel(
                     rhs_scale=w_scales[:, DI * q : DI * q + 512],
                     start=(q == 0), stop=(q == QUADS - 1),
                 )
+            reached[g, j] = hi
             if hi == QUADS:
+                finished.append((g, j))
                 rows = out_0[512 * g : 512 * (g + 1), :].rearrange("(p j) d -> p j d", j=J)
                 evacuate(acc, rows[:, j, :], j)
 
         queues = {"half": [], "tq": [], "fq": [], "x": [], "grp": [], "wq": []}
 
         def queue_quad(g, q):
-            fz = dzp.tile([P, J, P, 4], BF16, name="fz", tag="fz", bufs=2, align_bytes=64)
             for h in range(2):
-                queues["half"].append(lambda h=h: quad_half(g, q, h, fz))
+                queues["half"].append(lambda h=h: quad_half(g, q, h))
             queues["tq"].append(lambda: quad_tokens(g, q))
-            queues["fq"].append(lambda: quad_features(g, q, fz))
+            queues["fq"].append(lambda: quad_features(g, q))
 
         def fetch(dmas):
             tile = stage.tile([P, J, DI], BF16, name="wr", tag="wr", bufs=2)
             for lo, hi, src in dmas:
-                nc.scalar.dma_start(out=tile[lo:hi, :, :], in_=src)
+                nc.gpsimd.dma_start(out=tile[lo:hi, :, :], in_=src)
             return tile
 
         def queue_operand(dmas, codes, scales, col):
@@ -403,8 +424,8 @@ def tile_share_lstm_cell_pa_v_kernel(
             "ff": lambda n: stt(st[n]["fc"], st[n]["fg"], -1.0, st[n]["fc"], ADD, MUL),
             "fcg": lambda n: stt(st[n]["ch"], st[n]["ch"], -1.0, st[n]["im"], ADD, MUL),
             "tau": lambda n: mul(new(n, "tau", vec), st[n]["tt"], m_bc[:, n // CHUNKS]),
-            "D2": v("D2", "g4f", -0.5, "tau", MUL, MUL),
-            "G": v("G", "g0s", -3.0, "g4f", MUL, ADD),
+            "D2": v("D2", "g4s", -0.5, "tau", MUL, MUL),
+            "G": v("G", "g0s", -3.0, "g4s", MUL, ADD),
             "E1": v("E1", "g3f", 1.5, "D2", MUL, ADD),
             "D1": v("D1", "E1", -1.0, "tau", MUL, MUL),
             "U": v("U", "D2", -1.0, "tau", MUL, MUL),
@@ -429,10 +450,9 @@ def tile_share_lstm_cell_pa_v_kernel(
         }
 
         def run(queue):
-            held = (queue == "grp" and queues["wq"]) or (
-                queue == "fq" and (2 * len(feat) + 2 > len(halves) or len(feat) == QUADS and (0, J - 1) not in accs))
-            if queue == "x" and stores:
-                stores.pop(0)()
+            held = (queue == "grp" and queues["wq"]) or (queue == "tq" and len(undone) > 4) or (
+                queue == "half" and len(halves) - 2 * len(feat) >= 4) or (
+                queue == "fq" and (2 * len(feat) + 2 > len(halves) or len(feat) == QUADS and len(finished) < J))
             if queues[queue] and not held:
                 queues[queue].pop(0)()
 
@@ -455,19 +475,21 @@ def tile_share_lstm_cell_pa_v_kernel(
                     steps[nm](1)
             for n in range(N + 1):
                 for nm, d in PERIOD:
-                    if nm in queues:
+                    if nm == "early":
+                        if n == N:
+                            for j in range(2):
+                                data_grad(1, j, len(feat) - QUADS)
+                    elif nm in queues:
                         if nm != "grp" or n > 0:
                             run(nm)
                     elif 0 <= n + d < N:
                         steps[nm](n + d)
             ending[0] = True
-            while stores:
-                stores.pop(0)()
             for nm in TAIL:
                 if nm[0] == "e":
-                    data_grad(1, int(nm[1]), 0, QUADS - 1)
-                elif nm[0] == "d":
                     data_grad(1, int(nm[1]), QUADS - 1)
+                elif nm[0] == "d":
+                    data_grad(1, int(nm[1]))
                 else:
                     run(nm)
             while queues["x"]:

from contextlib import ExitStack

import concourse.mybir as mybir
from concourse.masks import make_identity

F32 = mybir.dt.float32
BF16 = mybir.dt.bfloat16
U32 = mybir.dt.uint32
U8 = mybir.dt.uint8
E4M3 = mybir.dt.float8_e4m3fn_x4
E5M2 = mybir.dt.float8_e5m2_x4
ADD = mybir.AluOpType.add
SUB = mybir.AluOpType.subtract
MUL = mybir.AluOpType.mult
SIGMOID = mybir.ActivationFunctionType.Sigmoid
TANH = mybir.ActivationFunctionType.Tanh
SQUARE = mybir.ActivationFunctionType.Square
COPY = mybir.ActivationFunctionType.Copy

B, DI, DH, GATES = 1024, 384, 512, 7
P = 128
J = 4
W = 128
GROUPS = B // 512
CHUNKS = DH // W
UNITS = GATES * CHUNKS
QUADS = UNITS // 4
PAD = 128

FLOPS = 2 * 2 * B * GATES * DH * DI
BYTES = (
    B * 4 * DH * 4 + B * 3 * DH * 4 + 6 * B * DH * 2 + B * 2 + B * DI * 2 + GATES * DH * DI * 2
    + B * DI * 4 + GATES * DH * DI * 4
)

ORDER = [6, 5, 4, 2, 0, 1, 3]
K6 = (1.0 / 6.0) ** 0.5
K12 = (1.0 / 12.0) ** 0.5
N = GROUPS * CHUNKS
DG = 4
GR_BANKS, FLIP_BANKS, MX_BANKS = 1, 4, 2
PERIOD = [
    ("fcg", -1), ("PO", -1), ("ff", 0), ("half", 0), ("fgB", 0), ("t2", -1), ("grp", 0), ("tau", 0), ("P0", -1), ("x", 0),
    ("gb1", 0), ("G", 0), ("D2", 0), ("ldD", 1), ("gb0", 0), ("Fdo", -1), ("x", 0), ("b0", -1), ("E1", 0), ("gto", 0),
    ("qb1", 0), ("Fdtc", -1), ("Fb2", 0), ("ldA", 1), ("x", 0), ("fi", 0), ("tq", 0), ("fq", 0), ("D1", 0), ("tq", 0),
    ("ldC", 1), ("H1", 0), ("wq", 0), ("qb2", 0), ("x", 0), ("ldB", 1), ("gi", 1), ("fo", -1), ("bk", -1), ("x", 0),
    ("Fback", -1), ("gf", 1), ("half", 0), ("M", 0), ("Fh1", 0), ("U", 0), ("Fb1", 0), ("E0", 0), ("b2", 0), ("q", -1),
    ("P2", 0), ("df", -1), ("gch", 1), ("x", 0), ("grp", 0), ("chq", 0), ("im", 1), ("Fh0", 0), ("x", 0), ("di", -1),
    ("dc", -1), ("qo", 0), ("grp", 0), ("D0", 0), ("half", 0), ("qb0", 0), ("fgA", 1), ("P1", 0), ("x", 0), ("Fy", 0),
    ("wq", 0), ("tq", 0), ("wq", 0), ("b1", 0), ("ich", 1), ("x", 0), ("fc", 1), ("Fz", 1), ("tanh", 1), ("Fb0", 0),
    ("early", 0), ("fq", 0), ("x", 0), ("half", 0), ("NG", 0), ("gb2", 1),
]
HEAD = ["ldA", "ldB", "gi", "ldC", "fgB", "im", "gf", "gto", "fc", "gch", "ich", "gb0", "fgA", "Fz", "ldD", "tanh", "gb2", "qb0", "qb2", "chq", "fcg", "ff", "fi", "qo", "tau", "gb1", "qb1", "t2"]
TAIL = ["half", "fq", "d3", "x", "e3", "x", "x", "x", "d2", "x", "d0", "x", "half", "x", "tq", "e2", "e1", "x", "d1", "e0"]


def tile_share_lstm_cell_pa_v_kernel(
    tc, x, h_minors, c_minors, s0, s1, s2, mask, weight_ih, bias_ih, weight_hh, bias_hh,
    weight_sh0, bias_sh0, weight_sh1, bias_sh1, weight_sh2, bias_sh2,
    pre, pre_s, grad_0, grad_1, grad_2, grad_3, grad_4, out_0, out_1,
):
    nc = tc.nc
    with ExitStack() as ctx:
        keep = ctx.enter_context(tc.tile_pool(name="keep", bufs=1))
        raw = ctx.enter_context(tc.tile_pool(name="raw", bufs=2))
        act = ctx.enter_context(tc.tile_pool(name="act", bufs=2))
        vec = ctx.enter_context(tc.tile_pool(name="vec", bufs=1))
        dzp = ctx.enter_context(tc.tile_pool(name="dzp", bufs=2))
        stage = ctx.enter_context(tc.tile_pool(name="stage", bufs=1))
        gps = ctx.enter_context(tc.psum_pool(name="gps", bufs=GR_BANKS))
        fps = ctx.enter_context(tc.psum_pool(name="fps", bufs=FLIP_BANKS))
        aps = ctx.enter_context(tc.psum_pool(name="aps", bufs=1))
        mps = ctx.enter_context(tc.psum_pool(name="mps", bufs=MX_BANKS))

        ident = keep.tile([P, P], F32, name="ident")
        make_identity(nc, ident[:])
        ident_bf = keep.tile([P, P], BF16, name="ident_bf")
        make_identity(nc, ident_bf[:])
        warm = keep.tile([P, 1], F32, name="warm")
        nc.vector.memset(warm[:], 0.0)
        nc.scalar.activation(warm[:], warm[:], SIGMOID)

        w_codes = keep.tile([P, QUADS * DI + PAD], U32, name="w_codes", align_bytes=64)
        w_scales = keep.tile([P, QUADS * DI + PAD], U8, name="w_scales", align_bytes=64)
        x_codes = keep.tile([P, GROUPS * DI + PAD], U32, name="x_codes", align_bytes=64)
        x_scales = keep.tile([P, GROUPS * DI + PAD], U8, name="x_scales", align_bytes=64)
        for codes, scales, used in ((w_codes, w_scales, QUADS * DI), (x_codes, x_scales, GROUPS * DI)):
            nc.gpsimd.memset(codes[:, used : used + PAD], 0)
            nc.gpsimd.memset(scales[:, used : used + PAD], 0)

        m_raw = keep.tile([P, GROUPS, J], BF16, name="m_raw")
        m32 = keep.tile([P, GROUPS * J], F32, name="m32")
        m6 = keep.tile([P, GROUPS * J], F32, name="m6")
        m_bc = keep.tile([P, GROUPS, J, P], BF16, name="m_bc")

        def mcol(tile, g, j):
            return tile[:, g * J + j : g * J + j + 1]

        st = {n: {} for n in range(N)}

        def tokens(src, g, col0, width):
            return src[512 * g : 512 * (g + 1), col0 : col0 + width].rearrange("(p j) w -> p j w", j=J)

        LOADS = {
            "ldA": (("ig", pre, 0, F32), ("ch", pre, 3 * DH, F32), ("fg", pre, DH, F32), ("cm", c_minors, 0, BF16)),
            "ldB": (("g4", grad_4, 0, BF16), ("g0", grad_0, 0, BF16), ("g3", grad_3, 0, BF16), ("g2", grad_2, 0, BF16)),
            "ldC": (("tb1", pre_s, DH, F32), ("tb0", pre_s, 0, F32), ("tb2", pre_s, 2 * DH, F32),
                    ("to", pre, 2 * DH, F32)),
            "ldD": (("g1", grad_1, 0, BF16),),
        }

        def load(part):
            def step(n):
                if n % 2:
                    return
                g, c = divmod(n, CHUNKS)
                tiles = [(nm, src, col, raw.tile([P, J, 2 * W], dt, name=nm, tag=nm)) for nm, src, col, dt in LOADS[part]]
                for nm, src, col, tl in tiles:
                    st[n][nm] = tl[:, :, :W]
                    st[n + 1][nm] = tl[:, :, W:]
                    if n:
                        nc.sync.dma_start(out=tl[:], in_=tokens(src, g, col + c * W, 2 * W))
                    else:
                        nc.sync.dma_start(out=st[0][nm], in_=tokens(src, 0, col, W))
                if n == 0:
                    for nm, src, col, tl in tiles:
                        late.append(lambda nm=nm, src=src, col=col: nc.sync.dma_start(
                            out=st[1][nm], in_=tokens(src, 0, col + W, W)))
            return step

        late = []

        def new(n, nm, pool, dt=F32):
            tl = pool.tile([P, J, W], dt, name=nm, tag=nm)
            st[n][nm] = tl
            return tl

        def stt(out, a, s, b, op0, op1):
            nc.vector.scalar_tensor_tensor(out=out[:], in0=a[:], scalar=s, in1=b[:], op0=op0, op1=op1)

        def mul(out, a, b, op=MUL):
            nc.vector.tensor_tensor(out=out[:], in0=a[:], in1=b[:], op=op)

        def flip(n, nm, *terms):
            bank = fps.tile([P, J, P], F32, name="flipped", tag="flipped")
            for j in range(J):
                for i, term in enumerate(terms):
                    nc.tensor.matmul(
                        bank[:, j, :], lhsT=st[n][term][:, j, :], rhs=ident[:], is_transpose=True,
                        start=(i == 0), stop=(i == len(terms) - 1))
            st[n][nm] = bank

        def per_j(fn):
            for j in range(J):
                fn(j)

        def s_im(n):
            t = st[n]
            im = new(n, "im", act)
            per_j(lambda j: nc.scalar.activation(
                im[:, j, :], t["ig"][:, j, :], COPY, scale=mcol(m32, n // CHUNKS, j)))

        def s_gate(nm, fn, scale=1.0):
            return lambda n: nc.scalar.activation(st[n][nm], st[n][nm], fn, scale=scale)

        def s_square(nm, scale):
            return lambda n: nc.scalar.activation(new(n, "q" + nm, act)[:], st[n][nm], SQUARE, scale=scale)

        def s_oq(n):
            sq = new(n, "qto", act)
            nc.scalar.activation(sq[:], st[n]["to"], SQUARE, scale=K12)
            nc.scalar.activation(sq[:], sq[:], COPY, scale=-1.0, bias=1.0 / 12.0)

        def flip_pair(n, a, b):
            t = st[n]
            bank = gps.tile([P, 2, J, P], BF16, name="gb", tag="gb")
            for i, nm in enumerate((a, b)):
                for j in range(J):
                    nc.tensor.transpose(bank[:, i, j, :], t[nm][:, j, :], ident_bf[:])
                t[nm + "f"] = bank[:, i]
            if b == "g0":
                both = act.tile([P, 2, J, W], BF16, name="gs", tag="gs")
                nc.scalar.copy(both[:], bank[:])
                t["g4s"], t["g0s"] = both[:, 0], both[:, 1]

        quad_tiles = {}
        halves = []
        tok = {}
        feat = {}

        left = {}

        def unit_out(n, u):
            g, c = divmod(n, CHUNKS)
            q, kk = divmod(GATES * c + u, 4)
            if (g, q) not in quad_tiles:
                quad_tiles[g, q] = dzp.tile([P, 4, W, J], BF16, name="dz", tag="dz", bufs=3, align_bytes=64)
                left[g, q] = 4
            return quad_tiles[g, q][:, kk, :, :]

        def unit_done(n, u):
            g, c = divmod(n, CHUNKS)
            q = (GATES * c + u) // 4
            left[g, q] -= 1
            if left[g, q] == 0:
                queue_quad(g, q)

        def inter(tile):
            return tile[:].rearrange("p j w -> p w j")

        def final(n, u, sq, cst, val):
            nc.vector.scalar_tensor_tensor(
                out=unit_out(n, u), in0=inter(sq), scalar=cst, in1=inter(val), op0=ADD, op1=MUL)
            unit_done(n, u)

        def runs_of_four(tile):
            return tile[:].rearrange("p j (c i) -> p c j i", i=4)

        def final2(n, u, a, b):
            nc.vector.tensor_tensor(
                out=unit_out(n, u).rearrange("p (c i) j -> p c j i", i=4),
                in0=runs_of_four(a), in1=runs_of_four(b), op=MUL)
            unit_done(n, u)

        ending = [False]

        def copier(i):
            return nc.vector.tensor_copy if ending[0] and i % 2 else nc.scalar.copy

        fz_tiles = {}

        def quad_half(g, q, h):
            if h == 0:
                fz_tiles[g, q] = dzp.tile([P, J, P, 4], BF16, name="fz", tag="fz", bufs=2, align_bytes=64)
            fz = fz_tiles[g, q]
            words = quad_tiles[g, q][:].rearrange("p k w j -> p (k w j)").bitcast(F32)
            ps = mps.tile([P, 4, P], F32, name="mb", tag="mb")
            for t in range(4):
                nc.tensor.transpose(ps[:, t, :], words[:, 2 * t + h :: 8], ident[:])
            src = ps[:].rearrange("p t n -> p (t n)").bitcast(BF16).rearrange("p (t n e) -> p e n t", t=4, e=2)
            copier(h)(fz[:, 2 * h : 2 * h + 2, :, :], src)
            halves.append((g, q))

        def quad_tokens(g, q):
            nm = "%d_%d" % (g, q) if g == 0 else "1_%d" % (q % 2)
            tc_ = keep.tile([P, 4 * W], U32, name="tokc", tag="tokc" + nm, align_bytes=64)
            ts_ = keep.tile([P, 4 * W], U8, name="toks", tag="toks" + nm, align_bytes=64)
            tok[g, q] = (tc_, ts_)
            nc.vector.quantize_mx(
                out=tc_[:].bitcast(E5M2), scales=ts_[:],
                in_=quad_tiles[g, q][:].rearrange("p k w j -> p (k w j)"))
            if g == 1:
                for kk in range(4):
                    undone.append(kk)
                    queues["x"].append(lambda kk=kk: weight_grad(q, kk))

        def quad_features(g, q):
            fz = fz_tiles[g, q]
            fc_ = keep.tile([P, 4 * P], U32, name="featc", tag="featc%d" % q, align_bytes=64)
            fs_ = keep.tile([P, 4 * P], U8, name="feats", tag="feats%d" % q, align_bytes=64)
            feat[g, q] = (fc_, fs_)
            nc.vector.quantize_mx(
                out=fc_[:].bitcast(E5M2), scales=fs_[:], in_=fz[:].rearrange("p j n t -> p (j n t)"))
            if q == QUADS - 1 and g == 0:
                queues["x"][:0] = [
                    lambda j=j, hi=hi: data_grad(0, j, hi) for j in range(J) for hi in (DG, QUADS)]

        def evacuate(acc, dst, i):
            res = stage.tile([P, DI], F32, name="res", tag="res", bufs=4)
            copier(i)(res[:], acc[:, :DI])
            nc.sync.dma_start(out=dst, in_=res[:])

        undone = []

        def weight_grad(q, kk):
            undone.pop()
            c, u = divmod(4 * q + kk, GATES)
            row = DH * ORDER[u] + W * c
            acc = mps.tile([P, 512], F32, name="mb", tag="mb")
            for g in range(GROUPS):
                codes, scales = tok[g, q]
                nc.tensor.matmul_mx(
                    out=acc[:],
                    lhsT=codes[:, W * kk : W * (kk + 1)].bitcast(E5M2),
                    lhsT_scale=scales[:, W * kk : W * (kk + 1)],
                    rhs=x_codes[:, DI * g : DI * g + 512].bitcast(E4M3),
                    rhs_scale=x_scales[:, DI * g : DI * g + 512],
                    start=(g == 0), stop=(g == GROUPS - 1),
                )
            evacuate(acc, out_1[row : row + W, :], kk)

        accs = {}
        reached = {}
        finished = []

        def data_grad(g, j, hi=QUADS):
            lo = reached.get((g, j), 0)
            if lo == 0:
                pool, tag = (aps, "acc") if g == 0 or j == 0 else (gps, "gb") if j == 1 else (fps, "flipped")
                accs[g, j] = pool.tile([P, 512], F32, name=tag, tag=tag)
            acc = accs[g, j]
            for q in range(lo, hi):
                codes, scales = feat[g, q]
                nc.tensor.matmul_mx(
                    out=acc[:],
                    lhsT=codes[:, P * j : P * (j + 1)].bitcast(E5M2),
                    lhsT_scale=scales[:, P * j : P * (j + 1)],
                    rhs=w_codes[:, DI * q : DI * q + 512].bitcast(E4M3),
                    rhs_scale=w_scales[:, DI * q : DI * q + 512],
                    start=(q == 0), stop=(q == QUADS - 1),
                )
            reached[g, j] = hi
            if hi == QUADS:
                finished.append((g, j))
                rows = out_0[512 * g : 512 * (g + 1), :].rearrange("(p j) d -> p j d", j=J)
                evacuate(acc, rows[:, j, :], j)

        queues = {"half": [], "tq": [], "fq": [], "x": [], "grp": [], "wq": []}

        def queue_quad(g, q):
            for h in range(2):
                queues["half"].append(lambda h=h: quad_half(g, q, h))
            queues["tq"].append(lambda: quad_tokens(g, q))
            queues["fq"].append(lambda: quad_features(g, q))

        def fetch(dmas):
            tile = stage.tile([P, J, DI], BF16, name="wr", tag="wr", bufs=2)
            for lo, hi, src in dmas:
                nc.gpsimd.dma_start(out=tile[lo:hi, :, :], in_=src)
            return tile

        def queue_operand(dmas, codes, scales, col):
            tile = fetch(dmas)

            def group():
                if operands:
                    queue_operand(*operands.pop(0))
                grp = stage.tile([P, DI, J], BF16, name="grp", tag="grp", align_bytes=64)
                nc.scalar.copy(grp[:], tile[:].rearrange("p j d -> p d j"))
                flat = grp[:].rearrange("p d j -> p (d j)")

                def quantize():
                    for lo, hi in ((0, 256), (256, DI)):
                        nc.vector.quantize_mx(
                            out=codes[:, col + lo : col + hi].bitcast(E4M3), scales=scales[:, col + lo : col + hi],
                            in_=flat[:, 4 * lo : 4 * hi])

                queues["wq"].append(quantize)

            queues["grp"].append(group)

        def unit_rows(q, kk):
            c, u = divmod(4 * q + kk, GATES)
            row = DH * ORDER[u] + W * c
            return weight_ih[row : row + W, :].rearrange("(r j) d -> r j d", j=J)

        operands = [([(0, P, tokens(x, g, 0, DI))], x_codes, x_scales, DI * g) for g in range(GROUPS)]
        operands += [
            ([(32 * kk, 32 * kk + 32, unit_rows(q, kk)) for kk in range(4)], w_codes, w_scales, DI * q)
            for q in range(QUADS)
        ]

        def v_fc(n):
            t = st[n]
            fc = new(n, "fc", act)
            per_j(lambda j: nc.vector.scalar_tensor_tensor(
                out=fc[:, j, :], in0=t["fg"][:, j, :], scalar=mcol(m32, n // CHUNKS, j), in1=t["cm"][:, j, :],
                op0=MUL, op1=MUL))

        def v_q(n):
            t = st[n]
            qn = new(n, "qn", vec)
            per_j(lambda j: nc.vector.scalar_tensor_tensor(
                out=qn[:, j, :], in0=t["back"][:, j, :], scalar=mcol(m6, n // CHUNKS, j), in1=t["g1"][:, j, :],
                op0=MUL, op1=SUB))

        def v(nm, a, s, b, op0, op1):
            def step(n):
                stt(new(n, nm, vec), st[n][a], s, st[n][b], op0, op1)
            return step


        def v_over(nm, a, s, b, op0, op1):
            def step(n):
                stt(st[n][a], st[n][a], s, st[n][b], op0, op1)
                st[n][nm] = st[n][a]
            return step

        steps = {
            "gi": s_gate("ig", SIGMOID),
            "im": s_im,
            "gch": s_gate("ch", TANH),
            "gf": s_gate("fg", SIGMOID),
            "chq": s_gate("ch", SQUARE),
            "gb2": s_gate("tb2", TANH, 0.5),
            "gb1": s_gate("tb1", TANH, 0.5),
            "gb0": s_gate("tb0", TANH, 0.5),
            "gto": s_gate("to", TANH, -0.5),
            "qb2": s_square("tb2", K6),
            "qb1": s_square("tb1", K12),
            "qb0": s_square("tb0", K12),
            "qo": s_oq,
            "tanh": lambda n: nc.scalar.activation(new(n, "tt", act)[:], st[n]["zf"][:], TANH),
            "t2": lambda n: nc.scalar.activation(st[n]["tt"][:], st[n]["tt"][:], SQUARE),
            "ldA": load("ldA"),
            "ldB": load("ldB"),
            "ldC": load("ldC"),
            "ldD": load("ldD"),
            "fgA": lambda n: flip_pair(n, "g4", "g0"),
            "fgB": lambda n: flip_pair(n, "g3", "g2"),
            "Fz": lambda n: flip(n, "zf", "ich", "fc"),
            "Fb2": lambda n: flip(n, "b2", "D2"),
            "Fb1": lambda n: flip(n, "b1", "D1"),
            "Fb0": lambda n: flip(n, "b0", "D0"),
            "Fh1": lambda n: flip(n, "h1", "H1"),
            "Fh0": lambda n: flip(n, "h0", "E0", "M", "U"),
            "Fy": lambda n: flip(n, "y", "E0", "M", "U", "H1", "G"),
            "Fdo": lambda n: flip(n, "do", "NG", "D0", "D1"),
            "Fdtc": lambda n: flip(n, "dtc", "P0", "P1", "P2", "PO"),
            "Fback": lambda n: flip(n, "back", "bk"),
            "ich": lambda n: mul(new(n, "ich", act), st[n]["im"], st[n]["ch"]),
            "fc": v_fc,
            "fi": lambda n: stt(st[n]["ich"], st[n]["ig"], -1.0, st[n]["ich"], ADD, MUL),
            "ff": lambda n: stt(st[n]["fc"], st[n]["fg"], -1.0, st[n]["fc"], ADD, MUL),
            "fcg": lambda n: stt(st[n]["ch"], st[n]["ch"], -1.0, st[n]["im"], ADD, MUL),
            "tau": lambda n: mul(new(n, "tau", vec), st[n]["tt"], m_bc[:, n // CHUNKS]),
            "D2": v("D2", "g4s", -0.5, "tau", MUL, MUL),
            "G": v("G", "g0s", -3.0, "g4s", MUL, ADD),
            "E1": v("E1", "g3f", 1.5, "D2", MUL, ADD),
            "D1": v("D1", "E1", -1.0, "tau", MUL, MUL),
            "U": v("U", "D2", -1.0, "tau", MUL, MUL),
            "H1": lambda n: mul(new(n, "H1", vec), st[n]["E1"], st[n]["D2"], ADD),
            "M": v("M", "D2", 4.0, "D1", MUL, ADD),
            "NG": v("NG", "G", -1.0, "tau", MUL, MUL),
            "E0": v("E0", "g2f", 3.0, "M", MUL, ADD),
            "D0": v("D0", "E0", -1.0, "tau", MUL, MUL),
            "P0": v_over("P0", "tb0", 3.0, "h0", ADD, MUL),
            "P1": v_over("P1", "tb1", 5.0, "h1", ADD, MUL),
            "P2": v_over("P2", "tb2", 7.0, "g4", ADD, MUL),
            "PO": v_over("PO", "to", -1.0, "y", ADD, MUL),
            "bk": v_over("bk", "tt", -1.0, "dtc", ADD, MUL),
            "q": v_q,
            "b2": lambda n: final(n, 0, st[n]["qtb2"], -1.0 / 6.0, st[n]["b2"]),
            "b1": lambda n: final(n, 1, st[n]["qtb1"], -1.0 / 12.0, st[n]["b1"]),
            "b0": lambda n: final(n, 2, st[n]["qtb0"], -1.0 / 12.0, st[n]["b0"]),
            "fo": lambda n: final2(n, 3, st[n]["qto"], st[n]["do"]),
            "di": lambda n: final2(n, 4, st[n]["qn"], st[n]["ich"]),
            "df": lambda n: final2(n, 5, st[n]["qn"], st[n]["fc"]),
            "dc": lambda n: final2(n, 6, st[n]["qn"], st[n]["ch"]),
        }

        def run(queue):
            held = (queue == "grp" and queues["wq"]) or (queue == "tq" and len(undone) > 4) or (
                queue == "half" and len(halves) - 2 * len(feat) >= 4) or (
                queue == "fq" and (2 * len(feat) + 2 > len(halves) or len(feat) == QUADS and len(finished) < J))
            if queues[queue] and not held:
                queues[queue].pop(0)()

        with tc.manual_schedule():
            nc.sync.dma_start(out=m_raw[:], in_=mask.rearrange("(g p j) -> p g j", g=GROUPS, j=J))
            m_row = stage.tile([P, B], BF16, name="wr", tag="wr", bufs=2)
            nc.sync.dma_start(out=m_row[:], in_=mask.partition_broadcast(P))
            nc.vector.tensor_copy(out=m32[:], in_=m_raw[:].rearrange("p g j -> p (g j)"))
            nc.vector.tensor_scalar(out=m6[:], in0=m32[:], scalar1=1.0 / 6.0, scalar2=None, op0=MUL)
            nc.gpsimd.tensor_copy(out=m_bc[:], in_=m_row[:].rearrange("q (g p j) -> q g j p", g=GROUPS, j=J))
            early = [nm for nm, d in PERIOD if d > 0]
            for nm in HEAD:
                if nm in early:
                    steps[nm](0)
            for fn in late:
                fn()
            queue_operand(*operands.pop(0))
            for nm, d in PERIOD:
                if d == 2:
                    steps[nm](1)
            for n in range(N + 1):
                for nm, d in PERIOD:
                    if nm == "early":
                        if n == N:
                            for j in range(2):
                                data_grad(1, j, len(feat) - QUADS)
                    elif nm in queues:
                        if nm != "grp" or n > 0:
                            run(nm)
                    elif 0 <= n + d < N:
                        steps[nm](n + d)
            ending[0] = True
            for nm in TAIL:
                if nm[0] == "e":
                    data_grad(1, int(nm[1]), QUADS - 1)
                elif nm[0] == "d":
                    data_grad(1, int(nm[1]))
                else:
                    run(nm)
            while queues["x"]:
                run("x")
